import numpy as np
import ml_dtypes


def mxq(x, axis, fmt="e4m3"):
    dtype, down = {"e4m3": (ml_dtypes.float8_e4m3fn, 7), "e5m2": (ml_dtypes.float8_e5m2, 14)}[fmt]
    v = np.moveaxis(np.asarray(x, np.float32).astype(ml_dtypes.bfloat16).astype(np.float64), axis, -1)
    blocks = v.reshape(v.shape[:-1] + (-1, 32))
    amax = np.abs(blocks).max(-1, keepdims=True)
    byte = np.maximum(np.where(amax > 0, np.frexp(amax)[1] - 1 + 127, 0) - down, 1)
    scale = np.exp2(byte - 127.0)
    codes = (blocks / scale).astype(np.float32).astype(dtype).astype(np.float64)
    return np.moveaxis((codes * scale).reshape(v.shape), -1, axis)


WIDE = False


def mx_kscale(k):
    if not WIDE:
        return np.ones(k)
    levels = np.array([20, -20, 10, -10, 0])
    a = np.random.permutation(np.resize(levels, k // 512 * 4)).reshape(k // 512, 4)
    idx = np.arange(k)
    return np.exp2(a[idx // 512, idx % 128 // 32])


BF16 = ml_dtypes.bfloat16


def bf(x):
    return np.asarray(x, np.float32).astype(BF16)


def f64(x):
    return np.asarray(x).astype(np.float64)


N, DIN, DOUT = 4096, 1024, 1024
MIN_NORM = 1e-15
EPS_PROJ = 4e-3
MAXNORM = 1.0 - EPS_PROJ


def rsum(v):
    return np.sum(v, axis=-1, keepdims=True)


def safe_norm(v):
    return np.sqrt(np.maximum(rsum(v * v), MIN_NORM))


def artanh(u):
    u = np.clip(u, -1.0 + 1e-5, 1.0 - 1e-5)
    return 0.5 * np.log((1.0 + u) / (1.0 - u))


def project(v):
    norm = safe_norm(v)
    return np.where(norm > MAXNORM, v / norm * MAXNORM, v)


def project_bwd(v, g):
    norm = safe_norm(v)
    return np.where(norm > MAXNORM, (g - v * rsum(g * v) / (norm * norm)) * (MAXNORM / norm), g)


def expmap0(u):
    u_norm = safe_norm(u)
    return np.tanh(u_norm) * u / u_norm


def mobius_add(x, y):
    x2 = rsum(x * x)
    y2 = rsum(y * y)
    xy = rsum(x * y)
    num = (1.0 + 2.0 * xy + y2) * x + (1.0 - x2) * y
    denom = 1.0 + 2.0 * xy + x2 * y2
    return num / np.maximum(denom, MIN_NORM)


def setup_inputs():
    s = mx_kscale(N)[:, None]
    lim = 2.0 * np.sqrt(6.0 / (DIN + DOUT))
    m = np.random.standard_normal(DIN)
    g = np.random.standard_normal((N, DIN)) + 0.5 * m
    r = 0.3 + 0.68 * np.random.random_sample((N, 1))
    w0 = np.random.uniform(-lim, lim, (DOUT, DIN))
    wm = w0 @ m
    b = wm / np.linalg.norm(wm) + np.random.standard_normal(DOUT) / np.sqrt(DOUT)
    x0 = bf(g / np.linalg.norm(g, axis=-1, keepdims=True) * r)
    weight = bf(w0)
    bias = bf(0.35 * b)
    go = bf(16.0 * np.random.standard_normal((N, DOUT)) * np.exp2(np.random.randint(-12, 1, (N, 1))) / s)
    z = f64(x0) @ f64(weight).T
    xn = safe_norm(f64(x0))
    ratio = artanh(xn) / xn
    return {"x": bf(f64(x0) * s), "weight": weight, "bias": bias,
            "z": np.asarray(z, np.float32), "ratio": np.asarray(ratio, np.float32), "grad_out": go}


def reference(x, weight, bias, z, ratio, grad_out):
    m = f64(z)
    a = f64(ratio)
    g = f64(grad_out)
    n = safe_norm(m)
    e = m / n
    t = np.tanh(n * a)
    u = t * e
    p = project(u)
    hb = project(expmap0(f64(bias)[None, :]))
    x2 = rsum(p * p)
    y2 = rsum(hb * hb)
    xy = rsum(p * hb)
    ca = 1.0 + 2.0 * xy + y2
    cb = 1.0 - x2
    den = np.maximum(1.0 + 2.0 * xy + x2 * y2, MIN_NORM)
    v = (ca * p + cb * hb) / den
    dv = project_bwd(v, g)
    q = dv / den
    dden = -rsum(q * v)
    dca = rsum(q * p)
    dcb = rsum(q * hb)
    dp = ca * q + 2.0 * (dca + dden) * hb + 2.0 * (y2 * dden - dcb) * p
    du = project_bwd(u, dp)
    ed = rsum(e * du)
    dz = (t / n) * (du - e * ed) + a * (1.0 - t * t) * ed * e
    dz = np.where(np.all(m == 0, axis=-1, keepdims=True), 0.0, dz)
    return mxq(dz, 0, "e5m2").T @ mxq(f64(x), 0, "e4m3")

@@ -1,0 +1,524 @@
+import concourse.mybir as mybir
+from concourse.masks import make_identity
+
+F32 = mybir.dt.float32
+BF16 = mybir.dt.bfloat16
+U32 = mybir.dt.uint32
+U8 = mybir.dt.uint8
+E4M3X4 = mybir.dt.float8_e4m3fn_x4
+E5M2X4 = mybir.dt.float8_e5m2_x4
+ALU = mybir.AluOpType
+FUNC = mybir.ActivationFunctionType
+
+P = 128
+PACK = 4
+K_PASS = P * PACK
+TOKENS = 4096
+D_IN = 1024
+D_OUT = 1024
+CHUNKS = TOKENS // K_PASS
+ROWS = CHUNKS * PACK
+N_TILE = 512
+M_TILE = 128
+BANKS = 8
+X_HALF = D_IN // 2
+X_HALVES = 2 * CHUNKS
+WORD_BLOCKS = D_OUT // 2 // P
+PIECES = 3
+
+SWEEP = BANKS // (D_IN // N_TILE) * M_TILE
+LAST_PIECES = (256, 128, 128)
+
+Z_LEAD = 8
+LOAD_AHEAD = 4
+FLIP_AHEAD = 2
+FLIP_BANKS = 4
+EARLY = 4
+CHAIN_SHARE = 12
+X_ON_VECTOR = 64
+SCRATCH_TILES = 3
+assert EARLY == LOAD_AHEAD
+
+MAXNORM = 1.0 - 4e-3
+MAXNORM_SQ = MAXNORM * MAXNORM
+MIN_NORM = 1e-15
+TINY = 1e-30
+W_MID = (MAXNORM_SQ + 1.0) / 2.0
+SERIES = (
+    MAXNORM * W_MID ** -0.5,
+    MAXNORM * -0.5 * W_MID ** -1.5,
+    MAXNORM * 0.375 * W_MID ** -2.5,
+    MAXNORM * -0.3125 * W_MID ** -3.5,
+)
+
+FLOPS = 2 * TOKENS * D_IN * D_OUT
+BYTES = TOKENS * D_IN * 2 + TOKENS * D_OUT * (4 + 2) + TOKENS * 4 + D_OUT * 2 + D_OUT * D_IN * 4
+
+
+def tile_hyplinear_v_kernel(tc, x, weight, bias, z, ratio, grad_out, out):
+    nc = tc.nc
+    x_chunks = x.rearrange("(c p j) w -> c p j w", p=P, j=PACK)
+    z_chunks = z.rearrange("(c p j) w -> c p j w", p=P, j=PACK)
+    g_chunks = grad_out.rearrange("(c p j) w -> c p j w", p=P, j=PACK)
+
+    def mul(o, a, b):
+        nc.vector.tensor_tensor(out=o, in0=a, in1=b, op=ALU.mult)
+
+    def add(o, a, b):
+        nc.vector.tensor_tensor(out=o, in0=a, in1=b, op=ALU.add)
+
+    def sub(o, a, b):
+        nc.vector.tensor_tensor(out=o, in0=a, in1=b, op=ALU.subtract)
+
+    def affine(o, a, m, b):
+        nc.vector.tensor_scalar(out=o, in0=a, scalar1=m, scalar2=b, op0=ALU.mult, op1=ALU.add)
+
+    def with_const(o, a, c, op):
+        nc.vector.tensor_scalar(out=o, in0=a, scalar1=c, scalar2=None, op0=op)
+
+    def scaled_plus(o, a, m, b):
+        nc.vector.scalar_tensor_tensor(out=o, in0=a, scalar=m, in1=b, op0=ALU.mult, op1=ALU.add)
+
+    def shifted_times(o, a, c, b):
+        nc.vector.scalar_tensor_tensor(out=o, in0=a, scalar=c, in1=b, op0=ALU.add, op1=ALU.mult)
+
+    def dot(acc, a, b):
+        products = ring4.tile([P, D_OUT], F32, tag="wide", align_bytes=64)
+        nc.vector.scalar_tensor_tensor(
+            out=products[:], in0=a, scalar=1.0, in1=b, op0=ALU.mult, op1=ALU.mult, accum_out=acc
+        )
+
+    with tc.tile_pool(name="keep", bufs=1) as keep, tc.tile_pool(name="ring4", bufs=4) as ring4, tc.tile_pool(
+        name="ring3", bufs=3
+    ) as ring3, tc.tile_pool(name="ring2", bufs=2) as ring2, tc.psum_pool(
+        name="banks", bufs=1
+    ) as banks, tc.manual_schedule():
+        z_all = keep.tile([P, ROWS, D_OUT], F32)
+        x_codes = keep.tile([P, CHUNKS, D_IN], U32, align_bytes=64)
+        x_scales = keep.tile([P, CHUNKS, D_IN], U8, align_bytes=64)
+        hb = keep.tile([P, D_OUT], F32)
+        identity = keep.tile([P, P], F32)
+        hb_pieces = keep.tile([P, WORD_BLOCKS, 2, PIECES], BF16)
+        y2 = keep.tile([P, 1], F32)
+        one_plus_y2 = keep.tile([P, 1], F32)
+        two_y2 = keep.tile([P, 1], F32)
+        minus_two_y2 = keep.tile([P, 1], F32)
+
+        def for_each_row(name, copies):
+            fresh = keep.tile([P] + copies + [ROWS], F32, name=name)
+            return fresh[:]
+
+        ratio_rows = for_each_row("ratio_rows", [])
+        sum_zz = for_each_row("sum_zz", [])
+        sum_zh = for_each_row("sum_zh", [])
+        sums_g = for_each_row("sums_g", [2])
+        alpha = for_each_row("alpha", [])
+        factors = for_each_row("factors", [2, 2])
+        terms = for_each_row("terms", [2, 2])
+        beta_gamma = for_each_row("beta_gamma", [2])
+
+        pairs = []
+        for i in range(SCRATCH_TILES):
+            page = keep.tile([P, N_TILE // ROWS, ROWS], F32, name="page%d" % i, tag="scratch%d" % i, align_bytes=64)
+            pairs.extend([page[:, v : v + 2, :] for v in range(0, N_TILE // ROWS, 2)])
+
+        def next_pair():
+            pair = pairs[0]
+            pairs.remove(pair)
+            return pair
+
+        def next_two():
+            pair = next_pair()
+            return pair[:, 0, :], pair[:, 1, :]
+
+        def over_pair(a):
+            return a.unsqueeze(1).to_broadcast([P, 2, ROWS])
+
+        n, rn = next_two()
+        t, nonzero = next_two()
+        he, s = next_two()
+        radial, inside = next_two()
+        xy, x2 = next_two()
+        srn, ca = next_two()
+        den, rden = next_two()
+        amb, vv = next_two()
+        v_out, fac = next_two()
+        series, w_mu = next_two()
+        w_qv, k1 = next_two()
+        k2, rnfac = next_two()
+        sfac, rs = next_two()
+        as_b = next_pair()
+        cas = as_b[:, 0, :]
+        cb = as_b[:, 1, :]
+        hn = next_pair()
+        en = next_pair()
+        al = next_pair()
+
+        from_z = [
+            lambda: with_const(n, sum_zz, MIN_NORM, ALU.max),
+            lambda: nc.scalar.sqrt(n, n),
+            lambda: with_const(nonzero, sum_zz, 0.0, ALU.is_gt),
+            None,
+            lambda: mul(t, n, ratio_rows),
+            lambda: nc.scalar.activation(out=t, in_=t, func=FUNC.Tanh),
+            lambda: nc.vector.reciprocal(out=rn, in_=n),
+            lambda: mul(he, sum_zh, rn),
+            None,
+            lambda: with_const(s, t, MAXNORM, ALU.min),
+            lambda: with_const(inside, t, MAXNORM, ALU.is_le),
+            lambda: mul(xy, s, he),
+            lambda: mul(x2, s, s),
+            lambda: mul(srn, s, rn),
+            lambda: affine(ca, xy, 2.0, one_plus_y2[:, 0:1]),
+            lambda: affine(cb, x2, -1.0, 1.0),
+            lambda: affine(den, x2, y2[:, 0:1], 1.0),
+            lambda: mul(sfac, nonzero, srn),
+            lambda: scaled_plus(den, xy, 2.0, den),
+            lambda: sub(amb, ca, cb),
+            lambda: mul(radial, ratio_rows, cb),
+            lambda: with_const(den, den, MIN_NORM, ALU.max),
+            lambda: mul(cas, ca, s),
+            lambda: with_const(w_mu, amb, TINY, ALU.max),
+            lambda: nc.vector.reciprocal(out=rden, in_=den),
+            lambda: mul(radial, radial, inside),
+            lambda: nc.vector.reciprocal(out=w_mu, in_=w_mu),
+            lambda: with_const(k1, cb, one_plus_y2[:, 0:1], ALU.mult),
+            lambda: mul(vv, amb, rden),
+            lambda: with_const(k2, cb, minus_two_y2[:, 0:1], ALU.mult),
+            lambda: mul(w_mu, w_mu, rden),
+            lambda: sub(rs, radial, srn),
+            lambda: with_const(v_out, vv, MAXNORM_SQ, ALU.is_gt),
+            lambda: nc.vector.tensor_scalar(
+                out=fac, in0=vv, scalar1=MAXNORM_SQ, scalar2=-W_MID, op0=ALU.max, op1=ALU.add
+            ),
+            lambda: scaled_plus(k1, ca, -2.0, k1),
+            lambda: scaled_plus(k2, ca, one_plus_y2[:, 0:1], k2),
+            lambda: affine(series, fac, SERIES[3], SERIES[2]),
+            lambda: mul(w_mu, w_mu, v_out),
+            lambda: affine(w_qv, v_out, -1.0, 1.0),
+            lambda: mul(series, series, fac),
+            lambda: mul(k1, k1, w_mu),
+            lambda: mul(w_qv, w_qv, rden),
+            lambda: mul(k2, k2, w_mu),
+            lambda: shifted_times(series, series, SERIES[1], fac),
+            lambda: scaled_plus(k1, w_qv, -2.0, k1),
+            lambda: scaled_plus(k2, w_qv, two_y2[:, 0:1], k2),
+            lambda: shifted_times(fac, series, SERIES[0], rden),
+            lambda: mul(hn, over_pair(k1), as_b),
+            lambda: mul(k2, s, k2),
+            lambda: mul(rnfac, rn, fac),
+            lambda: mul(sfac, sfac, fac),
+            lambda: scaled_plus(hn[:, 0, :], s, 2.0, hn[:, 0, :]),
+            lambda: mul(en, over_pair(k2), as_b),
+            lambda: mul(alpha, sfac, ca),
+            lambda: mul(al, over_pair(he), hn),
+            lambda: scaled_plus(en[:, 1, :], s, 2.0, en[:, 1, :]),
+            lambda: mul(factors[:, 1], over_pair(sfac), hn),
+            lambda: add(al[:, 0, :], al[:, 0, :], ca),
+            lambda: mul(en, over_pair(radial), en),
+            lambda: mul(al, over_pair(rs), al),
+            lambda: sub(al, al, en),
+            lambda: mul(factors[:, 0], over_pair(rnfac), al),
+            lambda: mul(factors[:, :, 0, :], factors[:, :, 0, :], over_pair(rn)),
+        ]
+        dealt = [0]
+
+        def deal(count):
+            for i in range(count):
+                if dealt[0] == len(from_z):
+                    return
+                instruction = from_z[dealt[0]]
+                dealt[0] += 1
+                if instruction is None:
+                    return
+                instruction()
+
+        def scalars_from_g():
+            nc.vector.tensor_reduce(out=sums_g[:, 1, :], in_=gh_psum[:], axis=mybir.AxisListType.X, op=ALU.add)
+            mul(terms, factors, sums_g.unsqueeze(1).to_broadcast([P, 2, 2, ROWS]))
+            add(beta_gamma, terms[:, :, 0, :], terms[:, :, 1, :])
+
+        def load_z(r):
+            nc.sync.dma_start(out=z_all[:, r], in_=z_chunks[r // PACK, :, r % PACK])
+
+        g_rows = {}
+
+        def load_g(r):
+            if r % 2 == 0:
+                two_rows = ring3.tile([P, 2, D_OUT], BF16, tag="g", align_bytes=64)
+                g_rows[r] = two_rows[:, 0]
+                g_rows[r + 1] = two_rows[:, 1]
+            nc.sync.dma_start(out=g_rows[r], in_=g_chunks[r // PACK, :, r % PACK])
+
+        x_loaded = {}
+
+        def load_x(k):
+            x_rows = ring2.tile([P, PACK, X_HALF], BF16, tag="rows", align_bytes=64)
+            nc.sync.dma_start(out=x_rows[:], in_=x_chunks[k // 2, :, :, (k % 2) * X_HALF : (k % 2 + 1) * X_HALF])
+            x_loaded[k] = x_rows
+
+        def sums_of_z(r):
+            squares = ring3.tile([P, D_OUT], BF16, tag="small", align_bytes=64)
+            nc.scalar.activation(out=squares[:], in_=z_all[:, r], func=FUNC.Square, accum_out=sum_zz[:, r : r + 1])
+            dot(sum_zh[:, r : r + 1], z_all[:, r], hb[:])
+
+        flipped = {}
+
+        def flip_g(r):
+            g_words = g_rows[r].bitcast(F32)
+            in_psum = banks.tile([P, WORD_BLOCKS, P], F32, tag="bank%d" % (r % FLIP_BANKS))
+            for b in range(WORD_BLOCKS):
+                nc.tensor.transpose(in_psum[:, b, :], g_words[:, b * P : (b + 1) * P], identity[:])
+            flipped[r] = in_psum
+
+        def g_times_hb(r):
+            in_sbuf = ring3.tile([P, WORD_BLOCKS, P, 2], BF16, tag="small", align_bytes=64)
+            nc.scalar.copy(
+                out=in_sbuf[:].rearrange("q b p e -> q (b p e)"),
+                in_=flipped[r][:].rearrange("q b p -> q (b p)").bitcast(BF16),
+            )
+            for b in range(WORD_BLOCKS):
+                for e in range(2):
+                    nc.tensor.matmul(
+                        out=gh_psum[:, r, :],
+                        lhsT=in_sbuf[:, b, :, e],
+                        rhs=hb_pieces[:, b, e, :],
+                        start=(b == 0 and e == 0),
+                        stop=(b == WORD_BLOCKS - 1 and e == 1),
+                    )
+
+        def g_dot_z(r):
+            dot(sums_g[:, 0, r : r + 1], g_rows[r], z_all[:, r])
+
+        def lay_out(rows, width, on_vector):
+            laid_out = ring2.tile([P, width, PACK], BF16, tag="laid_out", align_bytes=64)
+            cut = width - on_vector
+            nc.scalar.copy(
+                out=laid_out[:, :cut].rearrange("p (w i) j -> p w j i", i=4),
+                in_=rows[:, :, :cut].rearrange("p j (w i) -> p w j i", i=4),
+            )
+            if on_vector:
+                nc.vector.tensor_copy(
+                    out=laid_out[:, cut:].rearrange("p (w i) j -> p w j i", i=4),
+                    in_=rows[:, :, cut:].rearrange("p j (w i) -> p w j i", i=4),
+                )
+            return laid_out[:].rearrange("p w j -> p (w j)")
+
+        x_laid_out = {}
+
+        def quantise_x(k):
+            x_cols = slice((k % 2) * X_HALF, (k % 2 + 1) * X_HALF)
+            nc.vector.quantize_mx(
+                out=x_codes[:, k // 2, x_cols].bitcast(E4M3X4), scales=x_scales[:, k // 2, x_cols], in_=x_laid_out[k]
+            )
+
+        panels = []
+        for first_col in range(0, D_OUT, SWEEP):
+            for c in range(CHUNKS):
+                panels.append((c, first_col, SWEEP))
+        panels.remove((CHUNKS - 1, D_OUT - SWEEP, SWEEP))
+        first_col = D_OUT - SWEEP
+        for width in LAST_PIECES:
+            panels.append((CHUNKS - 1, first_col, width))
+            first_col += width
+        g_panels = {}
+        partial = {}
+        dz_made = {}
+        dz_laid_out = {}
+        dz_quantised = {}
+
+        def load_g_panel(k):
+            c, col, width = panels[k]
+            g_panel = ring3.tile([P, PACK, width], BF16, tag="g", align_bytes=64)
+            nc.sync.dma_start(out=g_panel[:], in_=g_chunks[c, :, :, col : col + width])
+            g_panels[k] = g_panel
+
+        def gamma_hb(k):
+            c, col, width = panels[k]
+            for u in range(PACK // 2):
+                two_rows = ring4.tile([P, 2, width], F32, tag="wide", align_bytes=64)
+                for v in range(2):
+                    r = c * PACK + 2 * u + v
+                    nc.scalar.activation(
+                        out=two_rows[:, v], in_=hb[:, col : col + width], func=FUNC.Copy, scale=beta_gamma[:, 1, r : r + 1]
+                    )
+                    partial[(k, 2 * u + v)] = two_rows[:, v]
+
+        def make_dz(k):
+            c, col, width = panels[k]
+            dz_rows = ring2.tile([P, PACK, width], BF16, tag="rows", align_bytes=64)
+            for j in range(PACK):
+                r = c * PACK + j
+                scaled_plus(partial[(k, j)], z_all[:, r, col : col + width], beta_gamma[:, 0, r : r + 1], partial[(k, j)])
+            for j in range(PACK):
+                r = c * PACK + j
+                scaled_plus(dz_rows[:, j], g_panels[k][:, j], alpha[:, r : r + 1], partial[(k, j)])
+            dz_made[k] = dz_rows
+
+        def quantise_dz(k):
+            width = panels[k][2]
+            dz_codes = ring3.tile([P, width], U32, align_bytes=64)
+            dz_scales = ring3.tile([P, width], U8, align_bytes=64)
+            nc.vector.quantize_mx(out=dz_codes[:].bitcast(E5M2X4), scales=dz_scales[:], in_=dz_laid_out[k])
+            dz_quantised[k] = (dz_codes, dz_scales)
+
+        acc = {}
+        bank_holds = {}
+        banks_taken = [0]
+        complete = []
+        stored = [0]
+
+        def store(i, at_the_end):
+            row_tile, h = complete[i]
+            complete.remove(complete[i])
+            turn = stored[0]
+            stored[0] += 1
+            if at_the_end:
+                pool = (ring3, ring3, ring4, ring4)[turn % 4]
+                tag = ("small", "g", "wide", "wide")[turn % 4]
+            elif turn % 2 == 0:
+                pool = ring3
+                tag = "small"
+            else:
+                pool = keep
+                tag = "scratch%d" % (turn // 2 % SCRATCH_TILES)
+            result = pool.tile([M_TILE, N_TILE], F32, tag=tag, align_bytes=64)
+            if at_the_end and turn % 2 == 1:
+                nc.vector.tensor_copy(out=result[:], in_=acc[(row_tile, h)][:])
+            else:
+                nc.scalar.copy(out=result[:], in_=acc[(row_tile, h)][:])
+            nc.sync.dma_start(
+                out=out[row_tile * M_TILE : (row_tile + 1) * M_TILE, h * N_TILE : (h + 1) * N_TILE], in_=result[:]
+            )
+
+        def multiply(k, m_from, m_to):
+            c, col, width = panels[k]
+            dz_codes, dz_scales = dz_quantised[k]
+            for m in range(m_from, m_to):
+                m_cols = slice(m * M_TILE, (m + 1) * M_TILE)
+                row_tile = col // M_TILE + m
+                for h in range(D_IN // N_TILE):
+                    n_cols = slice(h * N_TILE, (h + 1) * N_TILE)
+                    if c == 0:
+                        bank = BANKS - 1 - banks_taken[0] % BANKS
+                        banks_taken[0] += 1
+                        if bank_holds.get(bank) in complete:
+                            store(complete.index(bank_holds[bank]), False)
+                        bank_holds[bank] = (row_tile, h)
+                        acc[(row_tile, h)] = banks.tile(
+                            [M_TILE, N_TILE], F32, name="acc%d_%d" % (row_tile, h), tag="bank%d" % bank
+                        )
+                    nc.tensor.matmul_mx(
+                        out=acc[(row_tile, h)][:],
+                        lhsT=dz_codes[:, m_cols].bitcast(E5M2X4),
+                        lhsT_scale=dz_scales[:, m_cols],
+                        rhs=x_codes[:, c, n_cols].bitcast(E4M3X4),
+                        rhs_scale=x_scales[:, c, n_cols],
+                        start=(c == 0),
+                        stop=(c == CHUNKS - 1),
+                    )
+
+        bias_cols = keep.tile([P, WORD_BLOCKS, 2], BF16)
+        nc.scalar.dma_start(out=bias_cols[:], in_=bias.rearrange("(b q e) -> q b e", q=P, e=2))
+        nc.scalar.dma_start(
+            out=ratio_rows.rearrange("p (c j) -> p c j", j=PACK),
+            in_=ratio.rearrange("(c p j) o -> p c (j o)", p=P, j=PACK),
+        )
+        warm = keep.tile([P, 1], F32)
+        nc.gpsimd.memset(warm[:], 1.0)
+        nc.scalar.sqrt(warm[:], warm[:])
+        bias_rows = ring2.tile([P, D_OUT], BF16, tag="laid_out", align_bytes=64)
+        nc.sync.dma_start(out=bias_rows[:], in_=bias.partition_broadcast(P))
+        for r in range(EARLY):
+            load_z(r)
+            load_g(r)
+        make_identity(nc, identity[:])
+        gh_psum = banks.tile([P, ROWS, PIECES], F32, tag="bank%d" % FLIP_BANKS)
+        bb = keep.tile([P, 1], F32)
+        dot(bb[:], bias_rows[:], bias_rows[:])
+        nb = keep.tile([P, 1], F32)
+        with_const(nb[:], bb[:], MIN_NORM, ALU.max)
+        nc.scalar.sqrt(nb[:], nb[:])
+        scale_b = keep.tile([P, 1], F32)
+        nc.scalar.activation(out=scale_b[:], in_=nb[:], func=FUNC.Tanh)
+        for r in range(EARLY):
+            flip_g(r)
+        for r in range(EARLY // 2):
+            g_dot_z(r)
+        with_const(scale_b[:], scale_b[:], MAXNORM, ALU.min)
+        nc.vector.reciprocal(out=nb[:], in_=nb[:])
+        mul(scale_b[:], scale_b[:], nb[:])
+        with_const(hb[:], bias_rows[:], scale_b[:], ALU.mult)
+        mul(y2[:], scale_b[:], scale_b[:])
+        mul(y2[:], y2[:], bb[:])
+        with_const(one_plus_y2[:], y2[:], 1.0, ALU.add)
+        with_const(two_y2[:], y2[:], 2.0, ALU.mult)
+        with_const(minus_two_y2[:], y2[:], -2.0, ALU.mult)
+        rest = keep.tile([P, WORD_BLOCKS, 2], F32)
+        with_const(rest[:], bias_cols[:], scale_b[:], ALU.mult)
+        for i in range(PIECES):
+            nc.vector.tensor_copy(out=hb_pieces[:, :, :, i], in_=rest[:])
+            if i + 1 < PIECES:
+                sub(rest[:], rest[:], hb_pieces[:, :, :, i])
+        for r in range(EARLY // 2, EARLY):
+            g_dot_z(r)
+
+        for step in range(ROWS + Z_LEAD):
+            rg = step - Z_LEAD
+            if step + LOAD_AHEAD < ROWS:
+                load_z(step + LOAD_AHEAD)
+            if EARLY <= rg + LOAD_AHEAD < ROWS:
+                load_g(rg + LOAD_AHEAD)
+            if rg + 3 >= 0 and rg % 2 == 0 and (rg + 3) // 2 < X_HALVES:
+                load_x((rg + 3) // 2)
+            if EARLY <= rg + FLIP_AHEAD < ROWS:
+                flip_g(rg + FLIP_AHEAD)
+            if step < ROWS:
+                sums_of_z(step)
+            else:
+                deal(CHAIN_SHARE)
+            if step < EARLY:
+                g_times_hb(step)
+            if rg >= EARLY:
+                g_times_hb(rg)
+                g_dot_z(rg)
+            if rg >= 0 and rg % 2 == 1:
+                x_laid_out[rg // 2] = lay_out(x_loaded[rg // 2], X_HALF, X_ON_VECTOR)
+            if rg >= 2 and rg % 2 == 0:
+                quantise_x(rg // 2 - 1)
+        assert dealt[0] == len(from_z)
+        scalars_from_g()
+        quantise_x(X_HALVES - 1)
+
+        load_g_panel(0)
+        load_g_panel(1)
+        gamma_hb(0)
+        put_off = []
+        for k in range(len(panels) + 1):
+            if k + 2 < len(panels):
+                load_g_panel(k + 2)
+            if k >= 1:
+                dz_laid_out[k - 1] = lay_out(dz_made[k - 1], panels[k - 1][2], 0)
+            if k + 1 < len(panels):
+                gamma_hb(k + 1)
+            if k < len(panels):
+                make_dz(k)
+            if k >= 1:
+                quantise_dz(k - 1)
+                c, col, width = panels[k - 1]
+                for late_k, m_from, m_to in put_off:
+                    multiply(late_k, m_from, m_to)
+                put_off.clear()
+                if c == 0 and len(complete) > 0:
+                    multiply(k - 1, 0, width // M_TILE // 2)
+                    put_off.append((k - 1, width // M_TILE // 2, width // M_TILE))
+                else:
+                    multiply(k - 1, 0, width // M_TILE)
+                    for i in range(len(complete)):
+                        store(0, True)
+                if c == CHUNKS - 1:
+                    for m in range(width // M_TILE):
+                        for h in range(D_IN // N_TILE):
+                            complete.append((col // M_TILE + m, h))
+        for i in range(len(complete)):
+            store(0, True)

@@ -36,6 +36,9 @@ FLIP_BANKS = 4
 EARLY = 4
 CHAIN_SHARE = 12
 X_ON_VECTOR = 64
+VIA_PSUM_TO = 24
+PASS_BANKS = 3
+X_ON_GPSIMD = 320
 SCRATCH_TILES = 3
 assert EARLY == LOAD_AHEAD
 
@@ -82,8 +85,11 @@ def tile_hyplinear_v_kernel(tc, x, weight, bias, z, ratio, grad_out, out):
     def shifted_times(o, a, c, b):
         nc.vector.scalar_tensor_tensor(out=o, in0=a, scalar=c, in1=b, op0=ALU.add, op1=ALU.mult)
 
-    def dot(acc, a, b):
-        products = ring4.tile([P, D_OUT], F32, tag="wide", align_bytes=64)
+    def dot(acc, a, b, spare_buffer=False):
+        if spare_buffer:
+            products = ring2.tile([P, D_OUT], F32, tag="laid_out", align_bytes=64)
+        else:
+            products = ring4.tile([P, D_OUT], F32, tag="wide", align_bytes=64)
         nc.vector.scalar_tensor_tensor(
             out=products[:], in0=a, scalar=1.0, in1=b, op0=ALU.mult, op1=ALU.mult, accum_out=acc
         )
@@ -98,6 +104,7 @@ def tile_hyplinear_v_kernel(tc, x, weight, bias, z, ratio, grad_out, out):
         x_scales = keep.tile([P, CHUNKS, D_IN], U8, align_bytes=64)
         hb = keep.tile([P, D_OUT], F32)
         identity = keep.tile([P, P], F32)
+        identity_bf = keep.tile([P, P], BF16)
         hb_pieces = keep.tile([P, WORD_BLOCKS, 2, PIECES], BF16)
         y2 = keep.tile([P, 1], F32)
         one_plus_y2 = keep.tile([P, 1], F32)
@@ -257,10 +264,10 @@ def tile_hyplinear_v_kernel(tc, x, weight, bias, z, ratio, grad_out, out):
             nc.sync.dma_start(out=x_rows[:], in_=x_chunks[k // 2, :, :, (k % 2) * X_HALF : (k % 2 + 1) * X_HALF])
             x_loaded[k] = x_rows
 
-        def sums_of_z(r):
+        def sums_of_z(r, spare_buffer=False):
             squares = ring3.tile([P, D_OUT], BF16, tag="small", align_bytes=64)
             nc.scalar.activation(out=squares[:], in_=z_all[:, r], func=FUNC.Square, accum_out=sum_zz[:, r : r + 1])
-            dot(sum_zh[:, r : r + 1], z_all[:, r], hb[:])
+            dot(sum_zh[:, r : r + 1], z_all[:, r], hb[:], spare_buffer)
 
         flipped = {}
 
@@ -272,7 +279,7 @@ def tile_hyplinear_v_kernel(tc, x, weight, bias, z, ratio, grad_out, out):
             flipped[r] = in_psum
 
         def g_times_hb(r):
-            in_sbuf = ring3.tile([P, WORD_BLOCKS, P, 2], BF16, tag="small", align_bytes=64)
+            in_sbuf = ring3.tile([P, WORD_BLOCKS, P, 2], BF16, tag="dz_codes", align_bytes=64)
             nc.scalar.copy(
                 out=in_sbuf[:].rearrange("q b p e -> q (b p e)"),
                 in_=flipped[r][:].rearrange("q b p -> q (b p)").bitcast(BF16),
@@ -287,12 +294,33 @@ def tile_hyplinear_v_kernel(tc, x, weight, bias, z, ratio, grad_out, out):
                         stop=(b == WORD_BLOCKS - 1 and e == 1),
                     )
 
-        def g_dot_z(r):
-            dot(sums_g[:, 0, r : r + 1], g_rows[r], z_all[:, r])
+        g_passed = {}
 
-        def lay_out(rows, width, on_vector):
+        def pass_g(r):
+            in_psum = banks.tile([P, D_OUT], BF16, name="passed%d" % r, tag="bank%d" % (FLIP_BANKS + 1 + r % PASS_BANKS))
+            for h in range(D_OUT // N_TILE):
+                cols = slice(h * N_TILE, (h + 1) * N_TILE)
+                nc.tensor.matmul(out=in_psum[:, cols], lhsT=identity_bf[:], rhs=g_rows[r][:, cols], start=True, stop=True)
+            g_passed[r] = in_psum
+
+        def g_dot_z(r):
+            if r in g_passed:
+                dot(sums_g[:, 0, r : r + 1], g_passed[r][:], z_all[:, r])
+            else:
+                dot(sums_g[:, 0, r : r + 1], g_rows[r], z_all[:, r])
+
+        def lay_out(rows, width, on_vector, on_gpsimd=0):
             laid_out = ring2.tile([P, width, PACK], BF16, tag="laid_out", align_bytes=64)
-            cut = width - on_vector
+            cut = width - on_vector - on_gpsimd
+            if on_gpsimd:
+                nc.gpsimd.tensor_scalar(
+                    out=laid_out[:, cut:],
+                    in0=rows[:, :, cut:].rearrange("p j w -> p w j"),
+                    scalar1=1.0,
+                    scalar2=0.0,
+                    op0=ALU.mult,
+                    op1=ALU.add,
+                )
             nc.scalar.copy(
                 out=laid_out[:, :cut].rearrange("p (w i) j -> p w j i", i=4),
                 in_=rows[:, :, :cut].rearrange("p j (w i) -> p w j i", i=4),
@@ -433,6 +461,7 @@ def tile_hyplinear_v_kernel(tc, x, weight, bias, z, ratio, grad_out, out):
             load_z(r)
             load_g(r)
         make_identity(nc, identity[:])
+        make_identity(nc, identity_bf[:])
         gh_psum = banks.tile([P, ROWS, PIECES], F32, tag="bank%d" % FLIP_BANKS)
         bb = keep.tile([P, 1], F32)
         dot(bb[:], bias_rows[:], bias_rows[:])
@@ -463,7 +492,7 @@ def tile_hyplinear_v_kernel(tc, x, weight, bias, z, ratio, grad_out, out):
         for r in range(EARLY // 2, EARLY):
             g_dot_z(r)
 
-        for step in range(ROWS + Z_LEAD):
+        def loads(step):
             rg = step - Z_LEAD
             if step + LOAD_AHEAD < ROWS:
                 load_z(step + LOAD_AHEAD)
@@ -471,20 +500,49 @@ def tile_hyplinear_v_kernel(tc, x, weight, bias, z, ratio, grad_out, out):
                 load_g(rg + LOAD_AHEAD)
             if rg + 3 >= 0 and rg % 2 == 0 and (rg + 3) // 2 < X_HALVES:
                 load_x((rg + 3) // 2)
+
+        for period in range(ROWS // 2):
+            z_pair = (2 * period, 2 * period + 1)
+            half = period - Z_LEAD // 2
+            g_pair = (2 * half, 2 * half + 1)
+            beside_gpsimd = EARLY <= g_pair[0] < VIA_PSUM_TO
+            for step in z_pair:
+                loads(step)
+            if beside_gpsimd:
+                for r in g_pair:
+                    pass_g(r)
+            for r in g_pair:
+                if EARLY <= r + FLIP_AHEAD < ROWS:
+                    flip_g(r + FLIP_AHEAD)
+            for r in z_pair:
+                if r < EARLY:
+                    g_times_hb(r)
+            for r in g_pair:
+                if r >= EARLY:
+                    g_times_hb(r)
+            sums_of_z(z_pair[0], beside_gpsimd)
+            sums_of_z(z_pair[1])
+            if half >= 1:
+                quantise_x(half - 1)
+            if half >= 0:
+                if beside_gpsimd:
+                    x_laid_out[half] = lay_out(x_loaded[half], X_HALF, 0, X_ON_GPSIMD)
+                else:
+                    x_laid_out[half] = lay_out(x_loaded[half], X_HALF, X_ON_VECTOR)
+            for r in g_pair:
+                if r >= EARLY:
+                    g_dot_z(r)
+        for step in range(ROWS, ROWS + Z_LEAD):
+            rg = step - Z_LEAD
+            loads(step)
             if EARLY <= rg + FLIP_AHEAD < ROWS:
                 flip_g(rg + FLIP_AHEAD)
-            if step < ROWS:
-                sums_of_z(step)
+            deal(CHAIN_SHARE)
+            g_times_hb(rg)
+            g_dot_z(rg)
+            if rg % 2 == 1:
+                x_laid_out[rg // 2] = lay_out(x_loaded[rg // 2], X_HALF, 0)
             else:
-                deal(CHAIN_SHARE)
-            if step < EARLY:
-                g_times_hb(step)
-            if rg >= EARLY:
-                g_times_hb(rg)
-                g_dot_z(rg)
-            if rg >= 0 and rg % 2 == 1:
-                x_laid_out[rg // 2] = lay_out(x_loaded[rg // 2], X_HALF, X_ON_VECTOR)
-            if rg >= 2 and rg % 2 == 0:
                 quantise_x(rg // 2 - 1)
         assert dealt[0] == len(from_z)
         scalars_from_g()

@@ -38,7 +38,7 @@ CHAIN_SHARE = 12
 X_ON_VECTOR = 64
 VIA_PSUM_TO = 24
 PASS_BANKS = 3
-X_ON_GPSIMD = 320
+X_ON_GPSIMD = 128
 SCRATCH_TILES = 3
 assert EARLY == LOAD_AHEAD
 

@@ -455,29 +455,45 @@ def tile_hyplinear_v_kernel(tc, x, weight, bias, z, ratio, grad_out, out):
         warm = keep.tile([P, 1], F32)
         nc.gpsimd.memset(warm[:], 1.0)
         nc.scalar.sqrt(warm[:], warm[:])
-        bias_rows = ring2.tile([P, D_OUT], BF16, tag="laid_out", align_bytes=64)
-        nc.sync.dma_start(out=bias_rows[:], in_=bias.partition_broadcast(P))
+        bias_one = ring2.tile([P, D_OUT], BF16, tag="laid_out", align_bytes=64)
+        nc.vector.memset(bias_one[:], 0.0)
+        nc.sync.dma_start(out=bias_one[0:1, :], in_=bias.rearrange("(o w) -> o w", o=1))
+        ones = keep.tile([P, P], BF16)
+        nc.gpsimd.memset(ones[:], 1.0)
         for r in range(EARLY):
             load_z(r)
             load_g(r)
         make_identity(nc, identity[:])
         make_identity(nc, identity_bf[:])
         gh_psum = banks.tile([P, ROWS, PIECES], F32, tag="bank%d" % FLIP_BANKS)
+        bias_spread = []
+        bb_halves = keep.tile([P, D_OUT // N_TILE], F32)
+        for h in range(D_OUT // N_TILE):
+            spread = banks.tile([P, N_TILE], F32, name="spread%d" % h, tag="bank%d" % (FLIP_BANKS + 1 + h))
+            nc.tensor.matmul(
+                out=spread[:], lhsT=ones[:], rhs=bias_one[:, h * N_TILE : (h + 1) * N_TILE], start=True, stop=True
+            )
+            bias_spread.append(spread)
+            squares = ring3.tile([P, N_TILE], BF16, tag="small", align_bytes=64)
+            nc.scalar.activation(out=squares[:], in_=spread[:], func=FUNC.Square, accum_out=bb_halves[:, h : h + 1])
+        for r in range(EARLY):
+            flip_g(r)
+        g_dot_z(0)
         bb = keep.tile([P, 1], F32)
-        dot(bb[:], bias_rows[:], bias_rows[:])
+        add(bb[:], bb_halves[:, 0:1], bb_halves[:, 1:2])
         nb = keep.tile([P, 1], F32)
         with_const(nb[:], bb[:], MIN_NORM, ALU.max)
         nc.scalar.sqrt(nb[:], nb[:])
         scale_b = keep.tile([P, 1], F32)
         nc.scalar.activation(out=scale_b[:], in_=nb[:], func=FUNC.Tanh)
-        for r in range(EARLY):
-            flip_g(r)
-        for r in range(EARLY // 2):
-            g_dot_z(r)
+        g_dot_z(1)
         with_const(scale_b[:], scale_b[:], MAXNORM, ALU.min)
         nc.vector.reciprocal(out=nb[:], in_=nb[:])
         mul(scale_b[:], scale_b[:], nb[:])
-        with_const(hb[:], bias_rows[:], scale_b[:], ALU.mult)
+        for h in range(D_OUT // N_TILE):
+            nc.scalar.activation(
+                out=hb[:, h * N_TILE : (h + 1) * N_TILE], in_=bias_spread[h][:], func=FUNC.Copy, scale=scale_b[:, 0:1]
+            )
         mul(y2[:], scale_b[:], scale_b[:])
         mul(y2[:], y2[:], bb[:])
         with_const(one_plus_y2[:], y2[:], 1.0, ALU.add)

@@ -39,6 +39,7 @@ X_ON_VECTOR = 64
 VIA_PSUM_TO = 24
 PASS_BANKS = 3
 X_ON_GPSIMD = 128
+RATIO_PERIOD = 10
 SCRATCH_TILES = 3
 assert EARLY == LOAD_AHEAD
 
@@ -448,10 +449,6 @@ def tile_hyplinear_v_kernel(tc, x, weight, bias, z, ratio, grad_out, out):
 
         bias_cols = keep.tile([P, WORD_BLOCKS, 2], BF16)
         nc.scalar.dma_start(out=bias_cols[:], in_=bias.rearrange("(b q e) -> q b e", q=P, e=2))
-        nc.scalar.dma_start(
-            out=ratio_rows.rearrange("p (c j) -> p c j", j=PACK),
-            in_=ratio.rearrange("(c p j) o -> p c (j o)", p=P, j=PACK),
-        )
         warm = keep.tile([P, 1], F32)
         nc.gpsimd.memset(warm[:], 1.0)
         nc.scalar.sqrt(warm[:], warm[:])
@@ -524,6 +521,11 @@ def tile_hyplinear_v_kernel(tc, x, weight, bias, z, ratio, grad_out, out):
             beside_gpsimd = EARLY <= g_pair[0] < VIA_PSUM_TO
             for step in z_pair:
                 loads(step)
+            if period == RATIO_PERIOD:
+                nc.scalar.dma_start(
+                    out=ratio_rows.rearrange("p (c j) -> p c j", j=PACK),
+                    in_=ratio.rearrange("(c p j) o -> p c (j o)", p=P, j=PACK),
+                )
             if beside_gpsimd:
                 for r in g_pair:
                     pass_g(r)

@@ -463,39 +463,39 @@ def tile_hyplinear_v_kernel(tc, x, weight, bias, z, ratio, grad_out, out):
         make_identity(nc, identity[:])
         make_identity(nc, identity_bf[:])
         gh_psum = banks.tile([P, ROWS, PIECES], F32, tag="bank%d" % FLIP_BANKS)
+        bb_part = keep.tile([P, 1], F32)
+        bias_squares = keep.tile([P, WORD_BLOCKS, 2], F32)
+        nc.vector.scalar_tensor_tensor(
+            out=bias_squares[:], in0=bias_cols[:], scalar=1.0, in1=bias_cols[:], op0=ALU.mult, op1=ALU.mult,
+            accum_out=bb_part[:],
+        )
+        bb_parts = banks.tile([P, P], F32, tag="bank%d" % (FLIP_BANKS + PASS_BANKS))
+        nc.tensor.transpose(bb_parts[:], bb_part[:, 0:1].to_broadcast([P, P]), identity[:])
         bias_spread = []
-        bb_halves = keep.tile([P, D_OUT // N_TILE], F32)
         for h in range(D_OUT // N_TILE):
             spread = banks.tile([P, N_TILE], F32, name="spread%d" % h, tag="bank%d" % (FLIP_BANKS + 1 + h))
             nc.tensor.matmul(
                 out=spread[:], lhsT=ones[:], rhs=bias_one[:, h * N_TILE : (h + 1) * N_TILE], start=True, stop=True
             )
             bias_spread.append(spread)
-            squares = ring3.tile([P, N_TILE], BF16, tag="small", align_bytes=64)
-            nc.scalar.activation(out=squares[:], in_=spread[:], func=FUNC.Square, accum_out=bb_halves[:, h : h + 1])
         for r in range(EARLY):
             flip_g(r)
-        g_dot_z(0)
         bb = keep.tile([P, 1], F32)
-        add(bb[:], bb_halves[:, 0:1], bb_halves[:, 1:2])
+        nc.vector.tensor_reduce(out=bb[:], in_=bb_parts[:], axis=mybir.AxisListType.X, op=ALU.add)
         nb = keep.tile([P, 1], F32)
         with_const(nb[:], bb[:], MIN_NORM, ALU.max)
         nc.scalar.sqrt(nb[:], nb[:])
         scale_b = keep.tile([P, 1], F32)
         nc.scalar.activation(out=scale_b[:], in_=nb[:], func=FUNC.Tanh)
+        g_dot_z(0)
+        rnb = keep.tile([P, 1], F32)
+        nc.vector.reciprocal(out=rnb[:], in_=nb[:])
         g_dot_z(1)
-        with_const(scale_b[:], scale_b[:], MAXNORM, ALU.min)
-        nc.vector.reciprocal(out=nb[:], in_=nb[:])
-        mul(scale_b[:], scale_b[:], nb[:])
-        for h in range(D_OUT // N_TILE):
-            nc.scalar.activation(
-                out=hb[:, h * N_TILE : (h + 1) * N_TILE], in_=bias_spread[h][:], func=FUNC.Copy, scale=scale_b[:, 0:1]
-            )
-        mul(y2[:], scale_b[:], scale_b[:])
-        mul(y2[:], y2[:], bb[:])
-        with_const(one_plus_y2[:], y2[:], 1.0, ALU.add)
-        with_const(two_y2[:], y2[:], 2.0, ALU.mult)
-        with_const(minus_two_y2[:], y2[:], -2.0, ALU.mult)
+        nc.vector.tensor_scalar(
+            out=scale_b[:], in0=scale_b[:], scalar1=MAXNORM, scalar2=rnb[:, 0:1], op0=ALU.min, op1=ALU.mult
+        )
+        nc.scalar.activation(out=hb[:, :N_TILE], in_=bias_spread[0][:], func=FUNC.Copy, scale=scale_b[:, 0:1])
+        with_const(hb[:, N_TILE:], bias_spread[1][:], scale_b[:, 0:1], ALU.mult)
         rest = keep.tile([P, WORD_BLOCKS, 2], F32)
         with_const(rest[:], bias_cols[:], scale_b[:], ALU.mult)
         for i in range(PIECES):
@@ -504,6 +504,11 @@ def tile_hyplinear_v_kernel(tc, x, weight, bias, z, ratio, grad_out, out):
                 sub(rest[:], rest[:], hb_pieces[:, :, :, i])
         for r in range(EARLY // 2, EARLY):
             g_dot_z(r)
+        mul(y2[:], scale_b[:], scale_b[:])
+        mul(y2[:], y2[:], bb[:])
+        with_const(one_plus_y2[:], y2[:], 1.0, ALU.add)
+        with_const(two_y2[:], y2[:], 2.0, ALU.mult)
+        with_const(minus_two_y2[:], y2[:], -2.0, ALU.mult)
 
         def loads(step):
             rg = step - Z_LEAD

@@ -494,8 +494,15 @@ def tile_hyplinear_v_kernel(tc, x, weight, bias, z, ratio, grad_out, out):
         nc.vector.tensor_scalar(
             out=scale_b[:], in0=scale_b[:], scalar1=MAXNORM, scalar2=rnb[:, 0:1], op0=ALU.min, op1=ALU.mult
         )
-        nc.scalar.activation(out=hb[:, :N_TILE], in_=bias_spread[0][:], func=FUNC.Copy, scale=scale_b[:, 0:1])
-        with_const(hb[:, N_TILE:], bias_spread[1][:], scale_b[:, 0:1], ALU.mult)
+        for h in range(D_OUT // N_TILE):
+            nc.scalar.activation(
+                out=hb[:, h * N_TILE : (h + 1) * N_TILE], in_=bias_spread[h][:], func=FUNC.Copy, scale=scale_b[:, 0:1]
+            )
+        nc.scalar.square(y2[:], scale_b[:])
+        nc.scalar.activation(out=y2[:], in_=y2[:], func=FUNC.Copy, scale=bb[:, 0:1])
+        nc.scalar.add(one_plus_y2[:], y2[:], 1.0)
+        nc.scalar.mul(two_y2[:], y2[:], 2.0)
+        nc.scalar.mul(minus_two_y2[:], y2[:], -2.0)
         rest = keep.tile([P, WORD_BLOCKS, 2], F32)
         with_const(rest[:], bias_cols[:], scale_b[:], ALU.mult)
         for i in range(PIECES):
@@ -504,11 +511,6 @@ def tile_hyplinear_v_kernel(tc, x, weight, bias, z, ratio, grad_out, out):
                 sub(rest[:], rest[:], hb_pieces[:, :, :, i])
         for r in range(EARLY // 2, EARLY):
             g_dot_z(r)
-        mul(y2[:], scale_b[:], scale_b[:])
-        mul(y2[:], y2[:], bb[:])
-        with_const(one_plus_y2[:], y2[:], 1.0, ALU.add)
-        with_const(two_y2[:], y2[:], 2.0, ALU.mult)
-        with_const(minus_two_y2[:], y2[:], -2.0, ALU.mult)
 
         def loads(step):
             rg = step - Z_LEAD

@@ -34,7 +34,7 @@ LOAD_AHEAD = 4
 FLIP_AHEAD = 2
 FLIP_BANKS = 4
 EARLY = 4
-CHAIN_SHARE = 12
+CHAIN_SHARE = 14
 X_ON_VECTOR = 64
 VIA_PSUM_TO = 24
 PASS_BANKS = 3
@@ -241,10 +241,19 @@ def tile_hyplinear_v_kernel(tc, x, weight, bias, z, ratio, grad_out, out):
                     return
                 instruction()
 
-        def scalars_from_g():
-            nc.vector.tensor_reduce(out=sums_g[:, 1, :], in_=gh_psum[:], axis=mybir.AxisListType.X, op=ALU.add)
-            mul(terms, factors, sums_g.unsqueeze(1).to_broadcast([P, 2, 2, ROWS]))
-            add(beta_gamma, terms[:, :, 0, :], terms[:, :, 1, :])
+        def scalars_from_g(r_from, r_to, gh_pieces):
+            rows = slice(r_from, r_to)
+            return [
+                lambda: nc.vector.tensor_reduce(
+                    out=sums_g[:, 1, rows], in_=gh_pieces, axis=mybir.AxisListType.X, op=ALU.add
+                ),
+                lambda: mul(
+                    terms[:, :, :, rows],
+                    factors[:, :, :, rows],
+                    sums_g[:, :, rows].unsqueeze(1).to_broadcast([P, 2, 2, r_to - r_from]),
+                ),
+                lambda: add(beta_gamma[:, :, rows], terms[:, :, 0, rows], terms[:, :, 1, rows]),
+            ]
 
         def load_z(r):
             nc.sync.dma_start(out=z_all[:, r], in_=z_chunks[r // PACK, :, r % PACK])
@@ -271,6 +280,7 @@ def tile_hyplinear_v_kernel(tc, x, weight, bias, z, ratio, grad_out, out):
             dot(sum_zh[:, r : r + 1], z_all[:, r], hb[:], spare_buffer)
 
         flipped = {}
+        gh_of_row = {}
 
         def flip_g(r):
             g_words = g_rows[r].bitcast(F32)
@@ -288,7 +298,7 @@ def tile_hyplinear_v_kernel(tc, x, weight, bias, z, ratio, grad_out, out):
             for b in range(WORD_BLOCKS):
                 for e in range(2):
                     nc.tensor.matmul(
-                        out=gh_psum[:, r, :],
+                        out=gh_of_row[r],
                         lhsT=in_sbuf[:, b, :, e],
                         rhs=hb_pieces[:, b, e, :],
                         start=(b == 0 and e == 0),
@@ -304,11 +314,11 @@ def tile_hyplinear_v_kernel(tc, x, weight, bias, z, ratio, grad_out, out):
                 nc.tensor.matmul(out=in_psum[:, cols], lhsT=identity_bf[:], rhs=g_rows[r][:, cols], start=True, stop=True)
             g_passed[r] = in_psum
 
-        def g_dot_z(r):
+        def g_dot_z(r, spare_buffer=False):
             if r in g_passed:
                 dot(sums_g[:, 0, r : r + 1], g_passed[r][:], z_all[:, r])
             else:
-                dot(sums_g[:, 0, r : r + 1], g_rows[r], z_all[:, r])
+                dot(sums_g[:, 0, r : r + 1], g_rows[r], z_all[:, r], spare_buffer)
 
         def lay_out(rows, width, on_vector, on_gpsimd=0):
             laid_out = ring2.tile([P, width, PACK], BF16, tag="laid_out", align_bytes=64)
@@ -462,7 +472,9 @@ def tile_hyplinear_v_kernel(tc, x, weight, bias, z, ratio, grad_out, out):
             load_g(r)
         make_identity(nc, identity[:])
         make_identity(nc, identity_bf[:])
-        gh_psum = banks.tile([P, ROWS, PIECES], F32, tag="bank%d" % FLIP_BANKS)
+        gh_psum = banks.tile([P, ROWS - PACK, PIECES], F32, tag="bank%d" % FLIP_BANKS)
+        for r in range(ROWS - PACK):
+            gh_of_row[r] = gh_psum[:, r, :]
         bb_part = keep.tile([P, 1], F32)
         bias_squares = keep.tile([P, WORD_BLOCKS, 2], F32)
         nc.vector.scalar_tensor_tensor(
@@ -504,13 +516,28 @@ def tile_hyplinear_v_kernel(tc, x, weight, bias, z, ratio, grad_out, out):
         nc.scalar.mul(two_y2[:], y2[:], 2.0)
         nc.scalar.mul(minus_two_y2[:], y2[:], -2.0)
         rest = keep.tile([P, WORD_BLOCKS, 2], F32)
-        with_const(rest[:], bias_cols[:], scale_b[:], ALU.mult)
+
+        def round_off(i):
+            return lambda: nc.vector.tensor_copy(out=hb_pieces[:, :, :, i], in_=rest[:])
+
+        def take_off(i):
+            return lambda: sub(rest[:], rest[:], hb_pieces[:, :, :, i])
+
+        to_pieces = [lambda: with_const(rest[:], bias_cols[:], scale_b[:], ALU.mult)]
         for i in range(PIECES):
-            nc.vector.tensor_copy(out=hb_pieces[:, :, :, i], in_=rest[:])
+            to_pieces.append(round_off(i))
             if i + 1 < PIECES:
-                sub(rest[:], rest[:], hb_pieces[:, :, :, i])
+                to_pieces.append(take_off(i))
+        pieces_done = [0]
+
+        def next_of_pieces():
+            if pieces_done[0] < len(to_pieces):
+                to_pieces[pieces_done[0]]()
+                pieces_done[0] += 1
+
         for r in range(EARLY // 2, EARLY):
             g_dot_z(r)
+            next_of_pieces()
 
         def loads(step):
             rg = step - Z_LEAD
@@ -540,13 +567,15 @@ def tile_hyplinear_v_kernel(tc, x, weight, bias, z, ratio, grad_out, out):
                 if EARLY <= r + FLIP_AHEAD < ROWS:
                     flip_g(r + FLIP_AHEAD)
             for r in z_pair:
-                if r < EARLY:
-                    g_times_hb(r)
+                if EARLY <= r < 2 * EARLY:
+                    g_times_hb(r - EARLY)
             for r in g_pair:
                 if r >= EARLY:
                     g_times_hb(r)
             sums_of_z(z_pair[0], beside_gpsimd)
+            next_of_pieces()
             sums_of_z(z_pair[1])
+            next_of_pieces()
             if half >= 1:
                 quantise_x(half - 1)
             if half >= 0:
@@ -557,7 +586,11 @@ def tile_hyplinear_v_kernel(tc, x, weight, bias, z, ratio, grad_out, out):
             for r in g_pair:
                 if r >= EARLY:
                     g_dot_z(r)
-        for step in range(ROWS, ROWS + Z_LEAD):
+        assert pieces_done[0] == len(to_pieces)
+        gh_last = banks.tile([P, PACK, PIECES], F32, tag="bank%d" % (FLIP_BANKS + 1))
+        for j in range(PACK):
+            gh_of_row[ROWS - PACK + j] = gh_last[:, j, :]
+        for step in range(ROWS, ROWS + Z_LEAD - 2):
             rg = step - Z_LEAD
             loads(step)
             if EARLY <= rg + FLIP_AHEAD < ROWS:
@@ -570,12 +603,22 @@ def tile_hyplinear_v_kernel(tc, x, weight, bias, z, ratio, grad_out, out):
             else:
                 quantise_x(rg // 2 - 1)
         assert dealt[0] == len(from_z)
-        scalars_from_g()
-        quantise_x(X_HALVES - 1)
-
+        all_but_last = scalars_from_g(0, ROWS - PACK, gh_psum[:])
+        last_chunk = scalars_from_g(ROWS - PACK, ROWS, gh_last[:])
+        all_but_last[0]()
+        g_times_hb(ROWS - 2)
+        g_dot_z(ROWS - 2)
+        all_but_last[1]()
+        x_laid_out[X_HALVES - 1] = lay_out(x_loaded[X_HALVES - 1], X_HALF, 0)
+        quantise_x(X_HALVES - 2)
+        all_but_last[2]()
         load_g_panel(0)
         load_g_panel(1)
         gamma_hb(0)
+        g_times_hb(ROWS - 1)
+        g_dot_z(ROWS - 1, True)
+        quantise_x(X_HALVES - 1)
+
         put_off = []
         for k in range(len(panels) + 1):
             if k + 2 < len(panels):
@@ -586,6 +629,8 @@ def tile_hyplinear_v_kernel(tc, x, weight, bias, z, ratio, grad_out, out):
                 gamma_hb(k + 1)
             if k < len(panels):
                 make_dz(k)
+            if k < len(last_chunk):
+                last_chunk[k]()
             if k >= 1:
                 quantise_dz(k - 1)
                 c, col, width = panels[k - 1]

@@ -29,12 +29,12 @@ PIECES = 3
 SWEEP = BANKS // (D_IN // N_TILE) * M_TILE
 LAST_PIECES = (256, 128, 128)
 
-Z_LEAD = 8
+Z_LEAD = 12
 LOAD_AHEAD = 4
 FLIP_AHEAD = 2
 FLIP_BANKS = 4
 EARLY = 4
-CHAIN_SHARE = 14
+WIDE = 4
 X_ON_VECTOR = 64
 VIA_PSUM_TO = 24
 PASS_BANKS = 3
@@ -162,85 +162,6 @@ def tile_hyplinear_v_kernel(tc, x, weight, bias, z, ratio, grad_out, out):
         en = next_pair()
         al = next_pair()
 
-        from_z = [
-            lambda: with_const(n, sum_zz, MIN_NORM, ALU.max),
-            lambda: nc.scalar.sqrt(n, n),
-            lambda: with_const(nonzero, sum_zz, 0.0, ALU.is_gt),
-            None,
-            lambda: mul(t, n, ratio_rows),
-            lambda: nc.scalar.activation(out=t, in_=t, func=FUNC.Tanh),
-            lambda: nc.vector.reciprocal(out=rn, in_=n),
-            lambda: mul(he, sum_zh, rn),
-            None,
-            lambda: with_const(s, t, MAXNORM, ALU.min),
-            lambda: with_const(inside, t, MAXNORM, ALU.is_le),
-            lambda: mul(xy, s, he),
-            lambda: mul(x2, s, s),
-            lambda: mul(srn, s, rn),
-            lambda: affine(ca, xy, 2.0, one_plus_y2[:, 0:1]),
-            lambda: affine(cb, x2, -1.0, 1.0),
-            lambda: affine(den, x2, y2[:, 0:1], 1.0),
-            lambda: mul(sfac, nonzero, srn),
-            lambda: scaled_plus(den, xy, 2.0, den),
-            lambda: sub(amb, ca, cb),
-            lambda: mul(radial, ratio_rows, cb),
-            lambda: with_const(den, den, MIN_NORM, ALU.max),
-            lambda: mul(cas, ca, s),
-            lambda: with_const(w_mu, amb, TINY, ALU.max),
-            lambda: nc.vector.reciprocal(out=rden, in_=den),
-            lambda: mul(radial, radial, inside),
-            lambda: nc.vector.reciprocal(out=w_mu, in_=w_mu),
-            lambda: with_const(k1, cb, one_plus_y2[:, 0:1], ALU.mult),
-            lambda: mul(vv, amb, rden),
-            lambda: with_const(k2, cb, minus_two_y2[:, 0:1], ALU.mult),
-            lambda: mul(w_mu, w_mu, rden),
-            lambda: sub(rs, radial, srn),
-            lambda: with_const(v_out, vv, MAXNORM_SQ, ALU.is_gt),
-            lambda: nc.vector.tensor_scalar(
-                out=fac, in0=vv, scalar1=MAXNORM_SQ, scalar2=-W_MID, op0=ALU.max, op1=ALU.add
-            ),
-            lambda: scaled_plus(k1, ca, -2.0, k1),
-            lambda: scaled_plus(k2, ca, one_plus_y2[:, 0:1], k2),
-            lambda: affine(series, fac, SERIES[3], SERIES[2]),
-            lambda: mul(w_mu, w_mu, v_out),
-            lambda: affine(w_qv, v_out, -1.0, 1.0),
-            lambda: mul(series, series, fac),
-            lambda: mul(k1, k1, w_mu),
-            lambda: mul(w_qv, w_qv, rden),
-            lambda: mul(k2, k2, w_mu),
-            lambda: shifted_times(series, series, SERIES[1], fac),
-            lambda: scaled_plus(k1, w_qv, -2.0, k1),
-            lambda: scaled_plus(k2, w_qv, two_y2[:, 0:1], k2),
-            lambda: shifted_times(fac, series, SERIES[0], rden),
-            lambda: mul(hn, over_pair(k1), as_b),
-            lambda: mul(k2, s, k2),
-            lambda: mul(rnfac, rn, fac),
-            lambda: mul(sfac, sfac, fac),
-            lambda: scaled_plus(hn[:, 0, :], s, 2.0, hn[:, 0, :]),
-            lambda: mul(en, over_pair(k2), as_b),
-            lambda: mul(alpha, sfac, ca),
-            lambda: mul(al, over_pair(he), hn),
-            lambda: scaled_plus(en[:, 1, :], s, 2.0, en[:, 1, :]),
-            lambda: mul(factors[:, 1], over_pair(sfac), hn),
-            lambda: add(al[:, 0, :], al[:, 0, :], ca),
-            lambda: mul(en, over_pair(radial), en),
-            lambda: mul(al, over_pair(rs), al),
-            lambda: sub(al, al, en),
-            lambda: mul(factors[:, 0], over_pair(rnfac), al),
-            lambda: mul(factors[:, :, 0, :], factors[:, :, 0, :], over_pair(rn)),
-        ]
-        dealt = [0]
-
-        def deal(count):
-            for i in range(count):
-                if dealt[0] == len(from_z):
-                    return
-                instruction = from_z[dealt[0]]
-                dealt[0] += 1
-                if instruction is None:
-                    return
-                instruction()
-
         def scalars_from_g(r_from, r_to, gh_pieces):
             rows = slice(r_from, r_to)
             return [
@@ -254,6 +175,131 @@ def tile_hyplinear_v_kernel(tc, x, weight, bias, z, ratio, grad_out, out):
                 ),
                 lambda: add(beta_gamma[:, :, rows], terms[:, :, 0, rows], terms[:, :, 1, rows]),
             ]
+
+        gh_psum = banks.tile([P, ROWS - PACK, PIECES], F32, tag="bank%d" % FLIP_BANKS)
+        all_but_last = scalars_from_g(0, ROWS - PACK, gh_psum[:])
+
+        levels = [
+            None,
+            [
+                lambda: with_const(n, sum_zz, MIN_NORM, ALU.max),
+                lambda: nc.scalar.sqrt(n, n),
+                lambda: with_const(nonzero, sum_zz, 0.0, ALU.is_gt),
+            ],
+            None,
+            [
+                lambda: mul(t, n, ratio_rows),
+                lambda: nc.scalar.activation(out=t, in_=t, func=FUNC.Tanh),
+                lambda: nc.vector.reciprocal(out=rn, in_=n),
+            ],
+            None,
+            [
+                lambda: with_const(s, t, MAXNORM, ALU.min),
+                lambda: with_const(inside, t, MAXNORM, ALU.is_le),
+                lambda: mul(he, sum_zh, rn),
+            ],
+            [
+                lambda: mul(xy, s, he),
+                lambda: mul(x2, s, s),
+                lambda: mul(srn, s, rn),
+            ],
+            [
+                lambda: affine(den, x2, y2[:, 0:1], 1.0),
+                lambda: affine(cb, x2, -1.0, 1.0),
+                lambda: affine(ca, xy, 2.0, one_plus_y2[:, 0:1]),
+                lambda: mul(sfac, nonzero, srn),
+            ],
+            [
+                lambda: scaled_plus(den, xy, 2.0, den),
+                lambda: mul(radial, ratio_rows, cb),
+                lambda: sub(amb, ca, cb),
+                lambda: mul(cas, ca, s),
+            ],
+            [
+                lambda: with_const(den, den, MIN_NORM, ALU.max),
+                lambda: mul(radial, radial, inside),
+                lambda: with_const(w_mu, amb, TINY, ALU.max),
+            ],
+            [
+                lambda: nc.vector.reciprocal(out=rden, in_=den),
+                lambda: nc.vector.reciprocal(out=w_mu, in_=w_mu),
+                lambda: sub(rs, radial, srn),
+                lambda: with_const(k1, cb, one_plus_y2[:, 0:1], ALU.mult),
+            ],
+            [
+                lambda: mul(vv, amb, rden),
+                lambda: mul(w_mu, w_mu, rden),
+                lambda: with_const(k2, cb, minus_two_y2[:, 0:1], ALU.mult),
+                lambda: scaled_plus(k1, ca, -2.0, k1),
+            ],
+            [
+                lambda: with_const(v_out, vv, MAXNORM_SQ, ALU.is_gt),
+                lambda: nc.vector.tensor_scalar(
+                    out=fac, in0=vv, scalar1=MAXNORM_SQ, scalar2=-W_MID, op0=ALU.max, op1=ALU.add
+                ),
+                lambda: scaled_plus(k2, ca, one_plus_y2[:, 0:1], k2),
+            ],
+            [
+                lambda: affine(series, fac, SERIES[3], SERIES[2]),
+                lambda: mul(w_mu, w_mu, v_out),
+                lambda: affine(w_qv, v_out, -1.0, 1.0),
+            ],
+            [
+                lambda: mul(series, series, fac),
+                lambda: mul(w_qv, w_qv, rden),
+                lambda: mul(k1, k1, w_mu),
+                lambda: mul(k2, k2, w_mu),
+            ],
+            [
+                lambda: shifted_times(series, series, SERIES[1], fac),
+                lambda: scaled_plus(k1, w_qv, -2.0, k1),
+                lambda: scaled_plus(k2, w_qv, two_y2[:, 0:1], k2),
+            ],
+            [
+                lambda: shifted_times(fac, series, SERIES[0], rden),
+                lambda: mul(hn, over_pair(k1), as_b),
+                lambda: mul(k2, s, k2),
+            ],
+            [
+                lambda: scaled_plus(hn[:, 0, :], s, 2.0, hn[:, 0, :]),
+                lambda: mul(en, over_pair(k2), as_b),
+                lambda: mul(sfac, sfac, fac),
+                lambda: mul(rnfac, rn, fac),
+            ],
+            [
+                lambda: mul(al, over_pair(he), hn),
+                lambda: scaled_plus(en[:, 1, :], s, 2.0, en[:, 1, :]),
+                lambda: mul(alpha, sfac, ca),
+                lambda: mul(factors[:, 1], over_pair(sfac), hn),
+            ],
+            [
+                lambda: add(al[:, 0, :], al[:, 0, :], ca),
+                lambda: mul(en, over_pair(radial), en),
+            ],
+            [
+                lambda: mul(al, over_pair(rs), al),
+                all_but_last[0],
+            ],
+            [lambda: sub(al, al, en)],
+            [lambda: mul(factors[:, 0], over_pair(rnfac), al)],
+            [lambda: mul(factors[:, :, 0, :], factors[:, :, 0, :], over_pair(rn))],
+            [all_but_last[1]],
+            [all_but_last[2]],
+        ]
+        dealt = [0]
+
+        def next_levels():
+            for i in range(len(levels)):
+                if dealt[0] == len(levels):
+                    return
+                level = levels[dealt[0]]
+                dealt[0] += 1
+                if level is None:
+                    return
+                for instruction in level:
+                    instruction()
+                if len(level) < WIDE:
+                    return
 
         def load_z(r):
             nc.sync.dma_start(out=z_all[:, r], in_=z_chunks[r // PACK, :, r % PACK])
@@ -472,7 +518,6 @@ def tile_hyplinear_v_kernel(tc, x, weight, bias, z, ratio, grad_out, out):
             load_g(r)
         make_identity(nc, identity[:])
         make_identity(nc, identity_bf[:])
-        gh_psum = banks.tile([P, ROWS - PACK, PIECES], F32, tag="bank%d" % FLIP_BANKS)
         for r in range(ROWS - PACK):
             gh_of_row[r] = gh_psum[:, r, :]
         bb_part = keep.tile([P, 1], F32)
@@ -590,33 +635,28 @@ def tile_hyplinear_v_kernel(tc, x, weight, bias, z, ratio, grad_out, out):
         gh_last = banks.tile([P, PACK, PIECES], F32, tag="bank%d" % (FLIP_BANKS + 1))
         for j in range(PACK):
             gh_of_row[ROWS - PACK + j] = gh_last[:, j, :]
-        for step in range(ROWS, ROWS + Z_LEAD - 2):
+        last_chunk = scalars_from_g(ROWS - PACK, ROWS, gh_last[:])
+        for step in range(ROWS, ROWS + Z_LEAD):
             rg = step - Z_LEAD
             loads(step)
+            if rg == ROWS - 2:
+                load_g_panel(0)
+                load_g_panel(1)
             if EARLY <= rg + FLIP_AHEAD < ROWS:
                 flip_g(rg + FLIP_AHEAD)
-            deal(CHAIN_SHARE)
+            next_levels()
             g_times_hb(rg)
             g_dot_z(rg)
-            if rg % 2 == 1:
-                x_laid_out[rg // 2] = lay_out(x_loaded[rg // 2], X_HALF, 0)
-            else:
+            if rg % 2 == 0:
+                if rg == ROWS - 2:
+                    x_laid_out[X_HALVES - 1] = lay_out(x_loaded[X_HALVES - 1], X_HALF, 0)
+                next_levels()
                 quantise_x(rg // 2 - 1)
-        assert dealt[0] == len(from_z)
-        all_but_last = scalars_from_g(0, ROWS - PACK, gh_psum[:])
-        last_chunk = scalars_from_g(ROWS - PACK, ROWS, gh_last[:])
-        all_but_last[0]()
-        g_times_hb(ROWS - 2)
-        g_dot_z(ROWS - 2)
-        all_but_last[1]()
-        x_laid_out[X_HALVES - 1] = lay_out(x_loaded[X_HALVES - 1], X_HALF, 0)
-        quantise_x(X_HALVES - 2)
-        all_but_last[2]()
-        load_g_panel(0)
-        load_g_panel(1)
+            elif rg // 2 < X_HALVES - 1:
+                x_laid_out[rg // 2] = lay_out(x_loaded[rg // 2], X_HALF, 0)
+        next_levels()
+        assert dealt[0] == len(levels)
         gamma_hb(0)
-        g_times_hb(ROWS - 1)
-        g_dot_z(ROWS - 1, True)
         quantise_x(X_HALVES - 1)
 
         put_off = []

import concourse.mybir as mybir
from concourse.masks import make_identity

F32 = mybir.dt.float32
BF16 = mybir.dt.bfloat16
U32 = mybir.dt.uint32
U8 = mybir.dt.uint8
E4M3X4 = mybir.dt.float8_e4m3fn_x4
E5M2X4 = mybir.dt.float8_e5m2_x4
ALU = mybir.AluOpType
FUNC = mybir.ActivationFunctionType

P = 128
PACK = 4
K_PASS = P * PACK
TOKENS = 4096
D_IN = 1024
D_OUT = 1024
CHUNKS = TOKENS // K_PASS
ROWS = CHUNKS * PACK
N_TILE = 512
M_TILE = 128
BANKS = 8
X_HALF = D_IN // 2
X_HALVES = 2 * CHUNKS
WORD_BLOCKS = D_OUT // 2 // P
PIECES = 3

SWEEP = BANKS // (D_IN // N_TILE) * M_TILE
LAST_PIECES = (256, 128, 128)

Z_LEAD = 12
LOAD_AHEAD = 4
FLIP_AHEAD = 2
FLIP_BANKS = 4
EARLY = 4
WIDE = 4
X_ON_VECTOR = 64
VIA_PSUM_TO = 24
PASS_BANKS = 3
X_ON_GPSIMD = 128
RATIO_PERIOD = 10
SCRATCH_TILES = 3
assert EARLY == LOAD_AHEAD

MAXNORM = 1.0 - 4e-3
MAXNORM_SQ = MAXNORM * MAXNORM
MIN_NORM = 1e-15
TINY = 1e-30
W_MID = (MAXNORM_SQ + 1.0) / 2.0
SERIES = (
    MAXNORM * W_MID ** -0.5,
    MAXNORM * -0.5 * W_MID ** -1.5,
    MAXNORM * 0.375 * W_MID ** -2.5,
    MAXNORM * -0.3125 * W_MID ** -3.5,
)

FLOPS = 2 * TOKENS * D_IN * D_OUT
BYTES = TOKENS * D_IN * 2 + TOKENS * D_OUT * (4 + 2) + TOKENS * 4 + D_OUT * 2 + D_OUT * D_IN * 4


def tile_hyplinear_v_kernel(tc, x, weight, bias, z, ratio, grad_out, out):
    nc = tc.nc
    x_chunks = x.rearrange("(c p j) w -> c p j w", p=P, j=PACK)
    z_chunks = z.rearrange("(c p j) w -> c p j w", p=P, j=PACK)
    g_chunks = grad_out.rearrange("(c p j) w -> c p j w", p=P, j=PACK)

    def mul(o, a, b):
        nc.vector.tensor_tensor(out=o, in0=a, in1=b, op=ALU.mult)

    def add(o, a, b):
        nc.vector.tensor_tensor(out=o, in0=a, in1=b, op=ALU.add)

    def sub(o, a, b):
        nc.vector.tensor_tensor(out=o, in0=a, in1=b, op=ALU.subtract)

    def affine(o, a, m, b):
        nc.vector.tensor_scalar(out=o, in0=a, scalar1=m, scalar2=b, op0=ALU.mult, op1=ALU.add)

    def with_const(o, a, c, op):
        nc.vector.tensor_scalar(out=o, in0=a, scalar1=c, scalar2=None, op0=op)

    def scaled_plus(o, a, m, b):
        nc.vector.scalar_tensor_tensor(out=o, in0=a, scalar=m, in1=b, op0=ALU.mult, op1=ALU.add)

    def shifted_times(o, a, c, b):
        nc.vector.scalar_tensor_tensor(out=o, in0=a, scalar=c, in1=b, op0=ALU.add, op1=ALU.mult)

    def dot(acc, a, b, spare_buffer=False):
        if spare_buffer:
            products = ring2.tile([P, D_OUT], F32, tag="laid_out", align_bytes=64)
        else:
            products = ring4.tile([P, D_OUT], F32, tag="wide", align_bytes=64)
        nc.vector.scalar_tensor_tensor(
            out=products[:], in0=a, scalar=1.0, in1=b, op0=ALU.mult, op1=ALU.mult, accum_out=acc
        )

    with tc.tile_pool(name="keep", bufs=1) as keep, tc.tile_pool(name="ring4", bufs=4) as ring4, tc.tile_pool(
        name="ring3", bufs=3
    ) as ring3, tc.tile_pool(name="ring2", bufs=2) as ring2, tc.psum_pool(
        name="banks", bufs=1
    ) as banks, tc.manual_schedule():
        z_all = keep.tile([P, ROWS, D_OUT], F32)
        x_codes = keep.tile([P, CHUNKS, D_IN], U32, align_bytes=64)
        x_scales = keep.tile([P, CHUNKS, D_IN], U8, align_bytes=64)
        hb = keep.tile([P, D_OUT], F32)
        identity = keep.tile([P, P], F32)
        identity_bf = keep.tile([P, P], BF16)
        hb_pieces = keep.tile([P, WORD_BLOCKS, 2, PIECES], BF16)
        y2 = keep.tile([P, 1], F32)
        one_plus_y2 = keep.tile([P, 1], F32)
        two_y2 = keep.tile([P, 1], F32)
        minus_two_y2 = keep.tile([P, 1], F32)

        def for_each_row(name, copies):
            fresh = keep.tile([P] + copies + [ROWS], F32, name=name)
            return fresh[:]

        ratio_rows = for_each_row("ratio_rows", [])
        sum_zz = for_each_row("sum_zz", [])
        sum_zh = for_each_row("sum_zh", [])
        sums_g = for_each_row("sums_g", [2])
        alpha = for_each_row("alpha", [])
        factors = for_each_row("factors", [2, 2])
        terms = for_each_row("terms", [2, 2])
        beta_gamma = for_each_row("beta_gamma", [2])

        pairs = []
        for i in range(SCRATCH_TILES):
            page = keep.tile([P, N_TILE // ROWS, ROWS], F32, name="page%d" % i, tag="scratch%d" % i, align_bytes=64)
            pairs.extend([page[:, v : v + 2, :] for v in range(0, N_TILE // ROWS, 2)])

        def next_pair():
            pair = pairs[0]
            pairs.remove(pair)
            return pair

        def next_two():
            pair = next_pair()
            return pair[:, 0, :], pair[:, 1, :]

        def over_pair(a):
            return a.unsqueeze(1).to_broadcast([P, 2, ROWS])

        n, rn = next_two()
        t, nonzero = next_two()
        he, s = next_two()
        radial, inside = next_two()
        xy, x2 = next_two()
        srn, ca = next_two()
        den, rden = next_two()
        amb, vv = next_two()
        v_out, fac = next_two()
        series, w_mu = next_two()
        w_qv, k1 = next_two()
        k2, rnfac = next_two()
        sfac, rs = next_two()
        as_b = next_pair()
        cas = as_b[:, 0, :]
        cb = as_b[:, 1, :]
        hn = next_pair()
        en = next_pair()
        al = next_pair()

        def scalars_from_g(r_from, r_to, gh_pieces):
            rows = slice(r_from, r_to)
            return [
                lambda: nc.vector.tensor_reduce(
                    out=sums_g[:, 1, rows], in_=gh_pieces, axis=mybir.AxisListType.X, op=ALU.add
                ),
                lambda: mul(
                    terms[:, :, :, rows],
                    factors[:, :, :, rows],
                    sums_g[:, :, rows].unsqueeze(1).to_broadcast([P, 2, 2, r_to - r_from]),
                ),
                lambda: add(beta_gamma[:, :, rows], terms[:, :, 0, rows], terms[:, :, 1, rows]),
            ]

        gh_psum = banks.tile([P, ROWS - PACK, PIECES], F32, tag="bank%d" % FLIP_BANKS)
        all_but_last = scalars_from_g(0, ROWS - PACK, gh_psum[:])

        levels = [
            None,
            [
                lambda: with_const(n, sum_zz, MIN_NORM, ALU.max),
                lambda: nc.scalar.sqrt(n, n),
                lambda: with_const(nonzero, sum_zz, 0.0, ALU.is_gt),
            ],
            None,
            [
                lambda: mul(t, n, ratio_rows),
                lambda: nc.scalar.activation(out=t, in_=t, func=FUNC.Tanh),
                lambda: nc.vector.reciprocal(out=rn, in_=n),
            ],
            None,
            [
                lambda: with_const(s, t, MAXNORM, ALU.min),
                lambda: with_const(inside, t, MAXNORM, ALU.is_le),
                lambda: mul(he, sum_zh, rn),
            ],
            [
                lambda: mul(xy, s, he),
                lambda: mul(x2, s, s),
                lambda: mul(srn, s, rn),
            ],
            [
                lambda: affine(den, x2, y2[:, 0:1], 1.0),
                lambda: affine(cb, x2, -1.0, 1.0),
                lambda: affine(ca, xy, 2.0, one_plus_y2[:, 0:1]),
                lambda: mul(sfac, nonzero, srn),
            ],
            [
                lambda: scaled_plus(den, xy, 2.0, den),
                lambda: mul(radial, ratio_rows, cb),
                lambda: sub(amb, ca, cb),
                lambda: mul(cas, ca, s),
            ],
            [
                lambda: with_const(den, den, MIN_NORM, ALU.max),
                lambda: mul(radial, radial, inside),
                lambda: with_const(w_mu, amb, TINY, ALU.max),
            ],
            [
                lambda: nc.vector.reciprocal(out=rden, in_=den),
                lambda: nc.vector.reciprocal(out=w_mu, in_=w_mu),
                lambda: sub(rs, radial, srn),
                lambda: with_const(k1, cb, one_plus_y2[:, 0:1], ALU.mult),
            ],
            [
                lambda: mul(vv, amb, rden),
                lambda: mul(w_mu, w_mu, rden),
                lambda: with_const(k2, cb, minus_two_y2[:, 0:1], ALU.mult),
                lambda: scaled_plus(k1, ca, -2.0, k1),
            ],
            [
                lambda: with_const(v_out, vv, MAXNORM_SQ, ALU.is_gt),
                lambda: nc.vector.tensor_scalar(
                    out=fac, in0=vv, scalar1=MAXNORM_SQ, scalar2=-W_MID, op0=ALU.max, op1=ALU.add
                ),
                lambda: scaled_plus(k2, ca, one_plus_y2[:, 0:1], k2),
            ],
            [
                lambda: affine(series, fac, SERIES[3], SERIES[2]),
                lambda: mul(w_mu, w_mu, v_out),
                lambda: affine(w_qv, v_out, -1.0, 1.0),
            ],
            [
                lambda: mul(series, series, fac),
                lambda: mul(w_qv, w_qv, rden),
                lambda: mul(k1, k1, w_mu),
                lambda: mul(k2, k2, w_mu),
            ],
            [
                lambda: shifted_times(series, series, SERIES[1], fac),
                lambda: scaled_plus(k1, w_qv, -2.0, k1),
                lambda: scaled_plus(k2, w_qv, two_y2[:, 0:1], k2),
            ],
            [
                lambda: shifted_times(fac, series, SERIES[0], rden),
                lambda: mul(hn, over_pair(k1), as_b),
                lambda: mul(k2, s, k2),
            ],
            [
                lambda: scaled_plus(hn[:, 0, :], s, 2.0, hn[:, 0, :]),
                lambda: mul(en, over_pair(k2), as_b),
                lambda: mul(sfac, sfac, fac),
                lambda: mul(rnfac, rn, fac),
            ],
            [
                lambda: mul(al, over_pair(he), hn),
                lambda: scaled_plus(en[:, 1, :], s, 2.0, en[:, 1, :]),
                lambda: mul(alpha, sfac, ca),
                lambda: mul(factors[:, 1], over_pair(sfac), hn),
            ],
            [
                lambda: add(al[:, 0, :], al[:, 0, :], ca),
                lambda: mul(en, over_pair(radial), en),
            ],
            [
                lambda: mul(al, over_pair(rs), al),
                all_but_last[0],
            ],
            [lambda: sub(al, al, en)],
            [lambda: mul(factors[:, 0], over_pair(rnfac), al)],
            [lambda: mul(factors[:, :, 0, :], factors[:, :, 0, :], over_pair(rn))],
            [all_but_last[1]],
            [all_but_last[2]],
        ]
        dealt = [0]

        def next_levels():
            for i in range(len(levels)):
                if dealt[0] == len(levels):
                    return
                level = levels[dealt[0]]
                dealt[0] += 1
                if level is None:
                    return
                for instruction in level:
                    instruction()
                if len(level) < WIDE:
                    return

        def load_z(r):
            nc.sync.dma_start(out=z_all[:, r], in_=z_chunks[r // PACK, :, r % PACK])

        g_rows = {}

        def load_g(r):
            if r % 2 == 0:
                two_rows = ring3.tile([P, 2, D_OUT], BF16, tag="g", align_bytes=64)
                g_rows[r] = two_rows[:, 0]
                g_rows[r + 1] = two_rows[:, 1]
            nc.sync.dma_start(out=g_rows[r], in_=g_chunks[r // PACK, :, r % PACK])

        x_loaded = {}

        def load_x(k):
            x_rows = ring2.tile([P, PACK, X_HALF], BF16, tag="rows", align_bytes=64)
            nc.sync.dma_start(out=x_rows[:], in_=x_chunks[k // 2, :, :, (k % 2) * X_HALF : (k % 2 + 1) * X_HALF])
            x_loaded[k] = x_rows

        def sums_of_z(r, spare_buffer=False):
            squares = ring3.tile([P, D_OUT], BF16, tag="small", align_bytes=64)
            nc.scalar.activation(out=squares[:], in_=z_all[:, r], func=FUNC.Square, accum_out=sum_zz[:, r : r + 1])
            dot(sum_zh[:, r : r + 1], z_all[:, r], hb[:], spare_buffer)

        flipped = {}
        gh_of_row = {}

        def flip_g(r):
            g_words = g_rows[r].bitcast(F32)
            in_psum = banks.tile([P, WORD_BLOCKS, P], F32, tag="bank%d" % (r % FLIP_BANKS))
            for b in range(WORD_BLOCKS):
                nc.tensor.transpose(in_psum[:, b, :], g_words[:, b * P : (b + 1) * P], identity[:])
            flipped[r] = in_psum

        def g_times_hb(r):
            in_sbuf = ring3.tile([P, WORD_BLOCKS, P, 2], BF16, tag="dz_codes", align_bytes=64)
            nc.scalar.copy(
                out=in_sbuf[:].rearrange("q b p e -> q (b p e)"),
                in_=flipped[r][:].rearrange("q b p -> q (b p)").bitcast(BF16),
            )
            for b in range(WORD_BLOCKS):
                for e in range(2):
                    nc.tensor.matmul(
                        out=gh_of_row[r],
                        lhsT=in_sbuf[:, b, :, e],
                        rhs=hb_pieces[:, b, e, :],
                        start=(b == 0 and e == 0),
                        stop=(b == WORD_BLOCKS - 1 and e == 1),
                    )

        g_passed = {}

        def pass_g(r):
            in_psum = banks.tile([P, D_OUT], BF16, name="passed%d" % r, tag="bank%d" % (FLIP_BANKS + 1 + r % PASS_BANKS))
            for h in range(D_OUT // N_TILE):
                cols = slice(h * N_TILE, (h + 1) * N_TILE)
                nc.tensor.matmul(out=in_psum[:, cols], lhsT=identity_bf[:], rhs=g_rows[r][:, cols], start=True, stop=True)
            g_passed[r] = in_psum

        def g_dot_z(r, spare_buffer=False):
            if r in g_passed:
                dot(sums_g[:, 0, r : r + 1], g_passed[r][:], z_all[:, r])
            else:
                dot(sums_g[:, 0, r : r + 1], g_rows[r], z_all[:, r], spare_buffer)

        def lay_out(rows, width, on_vector, on_gpsimd=0):
            laid_out = ring2.tile([P, width, PACK], BF16, tag="laid_out", align_bytes=64)
            cut = width - on_vector - on_gpsimd
            if on_gpsimd:
                nc.gpsimd.tensor_scalar(
                    out=laid_out[:, cut:],
                    in0=rows[:, :, cut:].rearrange("p j w -> p w j"),
                    scalar1=1.0,
                    scalar2=0.0,
                    op0=ALU.mult,
                    op1=ALU.add,
                )
            nc.scalar.copy(
                out=laid_out[:, :cut].rearrange("p (w i) j -> p w j i", i=4),
                in_=rows[:, :, :cut].rearrange("p j (w i) -> p w j i", i=4),
            )
            if on_vector:
                nc.vector.tensor_copy(
                    out=laid_out[:, cut:].rearrange("p (w i) j -> p w j i", i=4),
                    in_=rows[:, :, cut:].rearrange("p j (w i) -> p w j i", i=4),
                )
            return laid_out[:].rearrange("p w j -> p (w j)")

        x_laid_out = {}

        def quantise_x(k):
            x_cols = slice((k % 2) * X_HALF, (k % 2 + 1) * X_HALF)
            nc.vector.quantize_mx(
                out=x_codes[:, k // 2, x_cols].bitcast(E4M3X4), scales=x_scales[:, k // 2, x_cols], in_=x_laid_out[k]
            )

        panels = []
        for first_col in range(0, D_OUT, SWEEP):
            for c in range(CHUNKS):
                panels.append((c, first_col, SWEEP))
        panels.remove((CHUNKS - 1, D_OUT - SWEEP, SWEEP))
        first_col = D_OUT - SWEEP
        for width in LAST_PIECES:
            panels.append((CHUNKS - 1, first_col, width))
            first_col += width
        g_panels = {}
        partial = {}
        dz_made = {}
        dz_laid_out = {}
        dz_quantised = {}

        def load_g_panel(k):
            c, col, width = panels[k]
            g_panel = ring3.tile([P, PACK, width], BF16, tag="g", align_bytes=64)
            nc.sync.dma_start(out=g_panel[:], in_=g_chunks[c, :, :, col : col + width])
            g_panels[k] = g_panel

        def gamma_hb(k):
            c, col, width = panels[k]
            for u in range(PACK // 2):
                two_rows = ring4.tile([P, 2, width], F32, tag="wide", align_bytes=64)
                for v in range(2):
                    r = c * PACK + 2 * u + v
                    nc.scalar.activation(
                        out=two_rows[:, v], in_=hb[:, col : col + width], func=FUNC.Copy, scale=beta_gamma[:, 1, r : r + 1]
                    )
                    partial[(k, 2 * u + v)] = two_rows[:, v]

        def make_dz(k):
            c, col, width = panels[k]
            dz_rows = ring2.tile([P, PACK, width], BF16, tag="rows", align_bytes=64)
            for j in range(PACK):
                r = c * PACK + j
                scaled_plus(partial[(k, j)], z_all[:, r, col : col + width], beta_gamma[:, 0, r : r + 1], partial[(k, j)])
            for j in range(PACK):
                r = c * PACK + j
                scaled_plus(dz_rows[:, j], g_panels[k][:, j], alpha[:, r : r + 1], partial[(k, j)])
            dz_made[k] = dz_rows

        def quantise_dz(k):
            width = panels[k][2]
            dz_codes = ring3.tile([P, width], U32, align_bytes=64)
            dz_scales = ring3.tile([P, width], U8, align_bytes=64)
            nc.vector.quantize_mx(out=dz_codes[:].bitcast(E5M2X4), scales=dz_scales[:], in_=dz_laid_out[k])
            dz_quantised[k] = (dz_codes, dz_scales)

        acc = {}
        bank_holds = {}
        banks_taken = [0]
        complete = []
        stored = [0]

        def store(i, at_the_end):
            row_tile, h = complete[i]
            complete.remove(complete[i])
            turn = stored[0]
            stored[0] += 1
            if at_the_end:
                pool = (ring3, ring3, ring4, ring4)[turn % 4]
                tag = ("small", "g", "wide", "wide")[turn % 4]
            elif turn % 2 == 0:
                pool = ring3
                tag = "small"
            else:
                pool = keep
                tag = "scratch%d" % (turn // 2 % SCRATCH_TILES)
            result = pool.tile([M_TILE, N_TILE], F32, tag=tag, align_bytes=64)
            if at_the_end and turn % 2 == 1:
                nc.vector.tensor_copy(out=result[:], in_=acc[(row_tile, h)][:])
            else:
                nc.scalar.copy(out=result[:], in_=acc[(row_tile, h)][:])
            nc.sync.dma_start(
                out=out[row_tile * M_TILE : (row_tile + 1) * M_TILE, h * N_TILE : (h + 1) * N_TILE], in_=result[:]
            )

        def multiply(k, m_from, m_to):
            c, col, width = panels[k]
            dz_codes, dz_scales = dz_quantised[k]
            for m in range(m_from, m_to):
                m_cols = slice(m * M_TILE, (m + 1) * M_TILE)
                row_tile = col // M_TILE + m
                for h in range(D_IN // N_TILE):
                    n_cols = slice(h * N_TILE, (h + 1) * N_TILE)
                    if c == 0:
                        bank = BANKS - 1 - banks_taken[0] % BANKS
                        banks_taken[0] += 1
                        if bank_holds.get(bank) in complete:
                            store(complete.index(bank_holds[bank]), False)
                        bank_holds[bank] = (row_tile, h)
                        acc[(row_tile, h)] = banks.tile(
                            [M_TILE, N_TILE], F32, name="acc%d_%d" % (row_tile, h), tag="bank%d" % bank
                        )
                    nc.tensor.matmul_mx(
                        out=acc[(row_tile, h)][:],
                        lhsT=dz_codes[:, m_cols].bitcast(E5M2X4),
                        lhsT_scale=dz_scales[:, m_cols],
                        rhs=x_codes[:, c, n_cols].bitcast(E4M3X4),
                        rhs_scale=x_scales[:, c, n_cols],
                        start=(c == 0),
                        stop=(c == CHUNKS - 1),
                    )

        bias_cols = keep.tile([P, WORD_BLOCKS, 2], BF16)
        nc.scalar.dma_start(out=bias_cols[:], in_=bias.rearrange("(b q e) -> q b e", q=P, e=2))
        warm = keep.tile([P, 1], F32)
        nc.gpsimd.memset(warm[:], 1.0)
        nc.scalar.sqrt(warm[:], warm[:])
        bias_one = ring2.tile([P, D_OUT], BF16, tag="laid_out", align_bytes=64)
        nc.vector.memset(bias_one[:], 0.0)
        nc.sync.dma_start(out=bias_one[0:1, :], in_=bias.rearrange("(o w) -> o w", o=1))
        ones = keep.tile([P, P], BF16)
        nc.gpsimd.memset(ones[:], 1.0)
        for r in range(EARLY):
            load_z(r)
            load_g(r)
        make_identity(nc, identity[:])
        make_identity(nc, identity_bf[:])
        for r in range(ROWS - PACK):
            gh_of_row[r] = gh_psum[:, r, :]
        bb_part = keep.tile([P, 1], F32)
        bias_squares = keep.tile([P, WORD_BLOCKS, 2], F32)
        nc.vector.scalar_tensor_tensor(
            out=bias_squares[:], in0=bias_cols[:], scalar=1.0, in1=bias_cols[:], op0=ALU.mult, op1=ALU.mult,
            accum_out=bb_part[:],
        )
        bb_parts = banks.tile([P, P], F32, tag="bank%d" % (FLIP_BANKS + PASS_BANKS))
        nc.tensor.transpose(bb_parts[:], bb_part[:, 0:1].to_broadcast([P, P]), identity[:])
        bias_spread = []
        for h in range(D_OUT // N_TILE):
            spread = banks.tile([P, N_TILE], F32, name="spread%d" % h, tag="bank%d" % (FLIP_BANKS + 1 + h))
            nc.tensor.matmul(
                out=spread[:], lhsT=ones[:], rhs=bias_one[:, h * N_TILE : (h + 1) * N_TILE], start=True, stop=True
            )
            bias_spread.append(spread)
        for r in range(EARLY):
            flip_g(r)
        bb = keep.tile([P, 1], F32)
        nc.vector.tensor_reduce(out=bb[:], in_=bb_parts[:], axis=mybir.AxisListType.X, op=ALU.add)
        nb = keep.tile([P, 1], F32)
        with_const(nb[:], bb[:], MIN_NORM, ALU.max)
        nc.scalar.sqrt(nb[:], nb[:])
        scale_b = keep.tile([P, 1], F32)
        nc.scalar.activation(out=scale_b[:], in_=nb[:], func=FUNC.Tanh)
        g_dot_z(0)
        rnb = keep.tile([P, 1], F32)
        nc.vector.reciprocal(out=rnb[:], in_=nb[:])
        g_dot_z(1)
        nc.vector.tensor_scalar(
            out=scale_b[:], in0=scale_b[:], scalar1=MAXNORM, scalar2=rnb[:, 0:1], op0=ALU.min, op1=ALU.mult
        )
        for h in range(D_OUT // N_TILE):
            nc.scalar.activation(
                out=hb[:, h * N_TILE : (h + 1) * N_TILE], in_=bias_spread[h][:], func=FUNC.Copy, scale=scale_b[:, 0:1]
            )
        nc.scalar.square(y2[:], scale_b[:])
        nc.scalar.activation(out=y2[:], in_=y2[:], func=FUNC.Copy, scale=bb[:, 0:1])
        nc.scalar.add(one_plus_y2[:], y2[:], 1.0)
        nc.scalar.mul(two_y2[:], y2[:], 2.0)
        nc.scalar.mul(minus_two_y2[:], y2[:], -2.0)
        rest = keep.tile([P, WORD_BLOCKS, 2], F32)

        def round_off(i):
            return lambda: nc.vector.tensor_copy(out=hb_pieces[:, :, :, i], in_=rest[:])

        def take_off(i):
            return lambda: sub(rest[:], rest[:], hb_pieces[:, :, :, i])

        to_pieces = [lambda: with_const(rest[:], bias_cols[:], scale_b[:], ALU.mult)]
        for i in range(PIECES):
            to_pieces.append(round_off(i))
            if i + 1 < PIECES:
                to_pieces.append(take_off(i))
        pieces_done = [0]

        def next_of_pieces():
            if pieces_done[0] < len(to_pieces):
                to_pieces[pieces_done[0]]()
                pieces_done[0] += 1

        for r in range(EARLY // 2, EARLY):
            g_dot_z(r)
            next_of_pieces()

        def loads(step):
            rg = step - Z_LEAD
            if step + LOAD_AHEAD < ROWS:
                load_z(step + LOAD_AHEAD)
            if EARLY <= rg + LOAD_AHEAD < ROWS:
                load_g(rg + LOAD_AHEAD)
            if rg + 3 >= 0 and rg % 2 == 0 and (rg + 3) // 2 < X_HALVES:
                load_x((rg + 3) // 2)

        for period in range(ROWS // 2):
            z_pair = (2 * period, 2 * period + 1)
            half = period - Z_LEAD // 2
            g_pair = (2 * half, 2 * half + 1)
            beside_gpsimd = EARLY <= g_pair[0] < VIA_PSUM_TO
            for step in z_pair:
                loads(step)
            if period == RATIO_PERIOD:
                nc.scalar.dma_start(
                    out=ratio_rows.rearrange("p (c j) -> p c j", j=PACK),
                    in_=ratio.rearrange("(c p j) o -> p c (j o)", p=P, j=PACK),
                )
            if beside_gpsimd:
                for r in g_pair:
                    pass_g(r)
            for r in g_pair:
                if EARLY <= r + FLIP_AHEAD < ROWS:
                    flip_g(r + FLIP_AHEAD)
            for r in z_pair:
                if EARLY <= r < 2 * EARLY:
                    g_times_hb(r - EARLY)
            for r in g_pair:
                if r >= EARLY:
                    g_times_hb(r)
            sums_of_z(z_pair[0], beside_gpsimd)
            next_of_pieces()
            sums_of_z(z_pair[1])
            next_of_pieces()
            if half >= 1:
                quantise_x(half - 1)
            if half >= 0:
                if beside_gpsimd:
                    x_laid_out[half] = lay_out(x_loaded[half], X_HALF, 0, X_ON_GPSIMD)
                else:
                    x_laid_out[half] = lay_out(x_loaded[half], X_HALF, X_ON_VECTOR)
            for r in g_pair:
                if r >= EARLY:
                    g_dot_z(r)
        assert pieces_done[0] == len(to_pieces)
        gh_last = banks.tile([P, PACK, PIECES], F32, tag="bank%d" % (FLIP_BANKS + 1))
        for j in range(PACK):
            gh_of_row[ROWS - PACK + j] = gh_last[:, j, :]
        last_chunk = scalars_from_g(ROWS - PACK, ROWS, gh_last[:])
        for step in range(ROWS, ROWS + Z_LEAD):
            rg = step - Z_LEAD
            loads(step)
            if rg == ROWS - 2:
                load_g_panel(0)
                load_g_panel(1)
            if EARLY <= rg + FLIP_AHEAD < ROWS:
                flip_g(rg + FLIP_AHEAD)
            next_levels()
            g_times_hb(rg)
            g_dot_z(rg)
            if rg % 2 == 0:
                if rg == ROWS - 2:
                    x_laid_out[X_HALVES - 1] = lay_out(x_loaded[X_HALVES - 1], X_HALF, 0)
                next_levels()
                quantise_x(rg // 2 - 1)
            elif rg // 2 < X_HALVES - 1:
                x_laid_out[rg // 2] = lay_out(x_loaded[rg // 2], X_HALF, 0)
        next_levels()
        assert dealt[0] == len(levels)
        gamma_hb(0)
        quantise_x(X_HALVES - 1)

        put_off = []
        for k in range(len(panels) + 1):
            if k + 2 < len(panels):
                load_g_panel(k + 2)
            if k >= 1:
                dz_laid_out[k - 1] = lay_out(dz_made[k - 1], panels[k - 1][2], 0)
            if k + 1 < len(panels):
                gamma_hb(k + 1)
            if k < len(panels):
                make_dz(k)
            if k < len(last_chunk):
                last_chunk[k]()
            if k >= 1:
                quantise_dz(k - 1)
                c, col, width = panels[k - 1]
                for late_k, m_from, m_to in put_off:
                    multiply(late_k, m_from, m_to)
                put_off.clear()
                if c == 0 and len(complete) > 0:
                    multiply(k - 1, 0, width // M_TILE // 2)
                    put_off.append((k - 1, width // M_TILE // 2, width // M_TILE))
                else:
                    multiply(k - 1, 0, width // M_TILE)
                    for i in range(len(complete)):
                        store(0, True)
                if c == CHUNKS - 1:
                    for m in range(width // M_TILE):
                        for h in range(D_IN // N_TILE):
                            complete.append((col // M_TILE + m, h))
        for i in range(len(complete)):
            store(0, True)
